import numpy as np
import ml_dtypes


def mxq(x, axis, fmt="e4m3"):
    dtype, down = {"e4m3": (ml_dtypes.float8_e4m3fn, 7), "e5m2": (ml_dtypes.float8_e5m2, 14)}[fmt]
    v = np.moveaxis(np.asarray(x, np.float32).astype(ml_dtypes.bfloat16).astype(np.float64), axis, -1)
    blocks = v.reshape(v.shape[:-1] + (-1, 32))
    amax = np.abs(blocks).max(-1, keepdims=True)
    byte = np.maximum(np.where(amax > 0, np.frexp(amax)[1] - 1 + 127, 0) - down, 1)
    scale = np.exp2(byte - 127.0)
    codes = (blocks / scale).astype(np.float32).astype(dtype).astype(np.float64)
    return np.moveaxis((codes * scale).reshape(v.shape), -1, axis)


WIDE = False


def mx_kscale(k):
    if not WIDE:
        return np.ones(k)
    levels = np.array([10, -10, 5, -5, 0])
    a = np.random.permutation(np.resize(levels, k // 512 * 4)).reshape(k // 512, 4)
    idx = np.arange(k)
    return np.exp2(a[idx // 512, idx % 128 // 32])


BF16 = ml_dtypes.bfloat16


def bf(x):
    return np.asarray(x, np.float32).astype(BF16)


def f64(x):
    return np.asarray(x).astype(np.float64)


B, D, L0, L1, L2 = 512, 8192, 32, 8192, 512
KC = L1 + D
LN_EPS = 1e-5


def log_softmax(v):
    sh = v - v.max(-1, keepdims=True)
    return sh - np.log(np.exp(sh).sum(-1, keepdims=True))


def setup_inputs():
    s = mx_kscale(D)
    w = np.random.standard_normal((L2, KC)) * 1.5 / np.sqrt(KC)
    w[:, L1:] /= s
    return {"mid_logits": bf(np.random.standard_normal((B, L1)) * 3.0), "x": bf(np.random.standard_normal((B, D)) * s),
            "W2": bf(w), "b2": bf(np.random.standard_normal(L2) * 0.5)}


def reference(mid_logits, x, W2, b2):
    h = np.maximum(f64(mid_logits), 0.0)
    mu = h.mean(-1, keepdims=True)
    var = h.var(-1, keepdims=True)
    hn = (h - mu) / np.sqrt(var + LN_EPS)
    c = np.concatenate([hn, f64(x)], axis=1)
    li = (mxq(c, 1, "e4m3") @ mxq(f64(W2), 1, "e4m3").T) + f64(b2)
    return log_softmax(li)

@@ -1,0 +1,179 @@
+from contextlib import ExitStack
+
+import concourse.mybir as mybir
+from concourse.masks import make_identity
+
+F32 = mybir.dt.float32
+BF16 = mybir.dt.bfloat16
+U32 = mybir.dt.uint32
+U8 = mybir.dt.uint8
+FP8X4 = mybir.dt.float8_e4m3fn_x4
+ACT = mybir.ActivationFunctionType
+ALU = mybir.AluOpType
+AX = mybir.AxisListType
+
+P = 128
+PACK = 4
+K_PASS = P * PACK
+WORDS_PASS = K_PASS // 2
+
+B = 512
+L1 = 8192
+D = 8192
+L2 = 512
+ROW_TILES = B // P
+CHUNK = 2048
+PASSES_CHUNK = CHUNK // K_PASS
+LN_EPS = 1e-5
+
+FLOPS = 2 * B * L2 * (L1 + D)
+
+
+def tile_bhcn_awx_pa_k_kernel(tc, mid_logits, x, W2, b2, out):
+    nc = tc.nc
+    with ExitStack() as stack:
+        const_pool = stack.enter_context(tc.tile_pool(name="const", bufs=1))
+        raw_pool = stack.enter_context(tc.tile_pool(name="raw", bufs=20))
+        norm_pool = stack.enter_context(tc.tile_pool(name="norm", bufs=1))
+        stat_pool = stack.enter_context(tc.tile_pool(name="stat", bufs=2))
+        scrap_pool = stack.enter_context(tc.tile_pool(name="scrap", bufs=2))
+        group_pool = stack.enter_context(tc.tile_pool(name="group", bufs=3))
+        code_pool = stack.enter_context(tc.tile_pool(name="code", bufs=3))
+        tail_pool = stack.enter_context(tc.tile_pool(name="tail", bufs=1))
+        acc_pool = stack.enter_context(tc.psum_pool(name="acc", bufs=1))
+        bank_pool = stack.enter_context(tc.psum_pool(name="bank", bufs=4))
+
+        ident = const_pool.tile([P, P], F32)
+        make_identity(nc, ident[:])
+
+        acc = [acc_pool.tile([P, L2], F32, name="acc%d" % rt) for rt in range(ROW_TILES)]
+
+        def load_chunk(src, rt, col0):
+            raw = raw_pool.tile([P, CHUNK], BF16, tag="raw")
+            nc.sync.dma_start(out=raw[:], in_=src[rt * P : (rt + 1) * P, col0 : col0 + CHUNK])
+            return raw
+
+        def prepare_pass(rows, word0, kind, copies):
+            grouped = group_pool.tile([P, B * PACK], BF16, align_bytes=64, tag="grouped_" + kind)
+            grouped_words = grouped[:].bitcast(F32)
+            for pair in range(2):
+                bank = bank_pool.tile([P, 2, 2, P], F32, tag="bank")
+                for a in range(2):
+                    words = rows[2 * pair + a][:].bitcast(F32)
+                    for u in range(2):
+                        first = word0 + u * P
+                        nc.tensor.transpose(bank[:, a, u, :], words[:, first : first + P], ident[:])
+                copies[pair](
+                    out=grouped_words[:, pair * 2 * 2 * P : (pair + 1) * 2 * 2 * P].rearrange(
+                        "p (a r u) -> p a r u", a=2, u=2
+                    ),
+                    in_=bank[:].rearrange("p a u r -> p a r u"),
+                )
+            codes = code_pool.tile([P, B], U32, align_bytes=64, tag="codes_" + kind)
+            scales = code_pool.tile([P, B], U8, align_bytes=64, tag="scales_" + kind)
+            nc.vector.quantize_mx(out=codes[:].bitcast(FP8X4), scales=scales[:], in_=grouped[:])
+            return codes, scales
+
+        def multiply_pass(c_mx, w_mx, first, last):
+            c_codes, c_scales = c_mx
+            w_codes, w_scales = w_mx
+            for rt in range(ROW_TILES):
+                cols = slice(rt * P, (rt + 1) * P)
+                nc.tensor.matmul_mx(
+                    out=acc[rt][:],
+                    lhsT=c_codes[:, cols].bitcast(FP8X4),
+                    lhsT_scale=c_scales[:, cols],
+                    rhs=w_codes[:].bitcast(FP8X4),
+                    rhs_scale=w_scales[:],
+                    start=first,
+                    stop=last,
+                )
+
+        def normalise(h):
+            sums = stat_pool.tile([P, L1 // CHUNK], F32)
+            for j in range(L1 // CHUNK):
+                cols = slice(j * CHUNK, (j + 1) * CHUNK)
+                nc.vector.tensor_scalar(
+                    out=h[:, cols], in0=h[:, cols], scalar1=0.0, scalar2=None,
+                    op0=ALU.max, op1=ALU.add, accum_out=sums[:, j : j + 1],
+                )
+            total = stat_pool.tile([P, 1], F32)
+            nc.vector.tensor_reduce(out=total[:], in_=sums[:], axis=AX.X, op=ALU.add)
+            neg_mean = stat_pool.tile([P, 1], F32)
+            nc.vector.tensor_scalar_mul(out=neg_mean[:], in0=total[:], scalar1=-1.0 / L1)
+            squares = stat_pool.tile([P, L1 // CHUNK], F32)
+            for j in range(L1 // CHUNK):
+                cols = slice(j * CHUNK, (j + 1) * CHUNK)
+                scrap = scrap_pool.tile([P, CHUNK], BF16)
+                nc.scalar.activation(
+                    out=scrap[:], in_=h[:, cols], func=ACT.Square, bias=neg_mean[:, 0:1], scale=1.0,
+                    accum_out=squares[:, j : j + 1],
+                )
+            spread = stat_pool.tile([P, 1], F32)
+            nc.vector.tensor_reduce(out=spread[:], in_=squares[:], axis=AX.X, op=ALU.add)
+            std = stat_pool.tile([P, 1], F32)
+            nc.scalar.activation(out=std[:], in_=spread[:], func=ACT.Sqrt, bias=LN_EPS, scale=1.0 / L1)
+            rstd = stat_pool.tile([P, 1], F32)
+            nc.vector.reciprocal(out=rstd[:], in_=std[:])
+            for j in range(L1 // CHUNK):
+                cols = slice(j * CHUNK, (j + 1) * CHUNK)
+                nc.vector.tensor_scalar(
+                    out=h[:, cols], in0=h[:, cols], scalar1=neg_mean[:, 0:1], scalar2=rstd[:, 0:1],
+                    op0=ALU.add, op1=ALU.mult,
+                )
+
+        to_scalar = nc.scalar.copy
+        to_vector = nc.vector.tensor_copy
+
+        hn = []
+        for q in range(D // CHUNK):
+            w_rows = [load_chunk(W2, rt, L1 + q * CHUNK) for rt in range(ROW_TILES)]
+            x_rows = [load_chunk(x, rt, q * CHUNK) for rt in range(ROW_TILES)]
+            h = norm_pool.tile([P, L1], BF16, name="h%d" % q)
+            for j in range(L1 // CHUNK):
+                cols = slice(j * CHUNK, (j + 1) * CHUNK)
+                nc.sync.dma_start(out=h[:, cols], in_=mid_logits[q * P : (q + 1) * P, cols])
+            hn.append(h)
+            for j in range(PASSES_CHUNK):
+                w_mx = prepare_pass(w_rows, j * WORDS_PASS, "w", (to_scalar, to_scalar))
+                c_mx = prepare_pass(x_rows, j * WORDS_PASS, "c", (to_scalar, to_vector))
+                multiply_pass(c_mx, w_mx, q == 0 and j == 0, False)
+            normalise(h)
+
+        bias = tail_pool.tile([P, L2], BF16)
+        nc.sync.dma_start(out=bias[:], in_=b2.partition_broadcast(P))
+
+        for q in range(L1 // CHUNK):
+            w_rows = [load_chunk(W2, rt, q * CHUNK) for rt in range(ROW_TILES)]
+            for j in range(PASSES_CHUNK):
+                g = q * PASSES_CHUNK + j
+                w_mx = prepare_pass(w_rows, j * WORDS_PASS, "w", (to_scalar, to_scalar))
+                c_mx = prepare_pass(hn, g * WORDS_PASS, "c", (to_scalar, to_vector))
+                multiply_pass(c_mx, w_mx, False, g == L1 // K_PASS - 1)
+
+        exp_sums = tail_pool.tile([P, ROW_TILES], F32)
+        logits = []
+        neg_maxes = []
+        for rt in range(ROW_TILES):
+            li = tail_pool.tile([P, L2], F32, name="li%d" % rt)
+            nc.vector.tensor_tensor(out=li[:], in0=acc[rt][:], in1=bias[:], op=ALU.add)
+            row_max = tail_pool.tile([P, 1], F32, name="row_max%d" % rt)
+            nc.vector.reduce_max(out=row_max[:], in_=li[:], axis=AX.X)
+            neg_max = tail_pool.tile([P, 1], F32, name="neg_max%d" % rt)
+            nc.vector.tensor_scalar_mul(out=neg_max[:], in0=row_max[:], scalar1=-1.0)
+            e = tail_pool.tile([P, L2], F32, name="e%d" % rt)
+            nc.scalar.activation(
+                out=e[:], in_=li[:], func=ACT.Exp, bias=neg_max[:, 0:1], scale=1.0,
+                accum_out=exp_sums[:, rt : rt + 1],
+            )
+            logits.append(li)
+            neg_maxes.append(neg_max)
+        log_sums = tail_pool.tile([P, ROW_TILES], F32)
+        nc.scalar.activation(out=log_sums[:], in_=exp_sums[:], func=ACT.Ln)
+        for rt in range(ROW_TILES):
+            li = logits[rt]
+            nc.vector.tensor_scalar(
+                out=li[:], in0=li[:], scalar1=neg_maxes[rt][:, 0:1], scalar2=log_sums[:, rt : rt + 1],
+                op0=ALU.add, op1=ALU.subtract,
+            )
+            nc.sync.dma_start(out=out[rt * P : (rt + 1) * P, :], in_=li[:])

@@ -23,8 +23,16 @@ D = 8192
 L2 = 512
 ROW_TILES = B // P
 CHUNK = 2048
+QUARTERS = L1 // CHUNK
 PASSES_CHUNK = CHUNK // K_PASS
+BLOCKS_STEP = 8
+BANKS_STEP = 4
 LN_EPS = 1e-5
+
+RELU_STEP0 = 2
+SQUARE_STEP0 = RELU_STEP0 + QUARTERS
+SCALE_STEP0 = SQUARE_STEP0 + QUARTERS
+NORM_SLICES = ROW_TILES * QUARTERS
 
 FLOPS = 2 * B * L2 * (L1 + D)
 
@@ -33,147 +41,221 @@ def tile_bhcn_awx_pa_k_kernel(tc, mid_logits, x, W2, b2, out):
     nc = tc.nc
     with ExitStack() as stack:
         const_pool = stack.enter_context(tc.tile_pool(name="const", bufs=1))
-        raw_pool = stack.enter_context(tc.tile_pool(name="raw", bufs=20))
+        raw_pool = stack.enter_context(tc.tile_pool(name="raw", bufs=16))
         norm_pool = stack.enter_context(tc.tile_pool(name="norm", bufs=1))
-        stat_pool = stack.enter_context(tc.tile_pool(name="stat", bufs=2))
         scrap_pool = stack.enter_context(tc.tile_pool(name="scrap", bufs=2))
-        group_pool = stack.enter_context(tc.tile_pool(name="group", bufs=3))
-        code_pool = stack.enter_context(tc.tile_pool(name="code", bufs=3))
+        group_pool = stack.enter_context(tc.tile_pool(name="group", bufs=2))
+        weight_pool = stack.enter_context(tc.tile_pool(name="weight", bufs=2 * QUARTERS))
+        rows_pool = stack.enter_context(tc.tile_pool(name="rows", bufs=3))
         tail_pool = stack.enter_context(tc.tile_pool(name="tail", bufs=1))
         acc_pool = stack.enter_context(tc.psum_pool(name="acc", bufs=1))
-        bank_pool = stack.enter_context(tc.psum_pool(name="bank", bufs=4))
+        bank_pool = stack.enter_context(tc.psum_pool(name="bank", bufs=BANKS_STEP))
+        stack.enter_context(tc.manual_schedule())
 
         ident = const_pool.tile([P, P], F32)
         make_identity(nc, ident[:])
+        one = const_pool.tile([P, 1], F32)
+        nc.vector.memset(one[:], 1.0)
+        warm = const_pool.tile([P, 1], F32)
+        nc.scalar.activation(out=warm[:], in_=one[:], func=ACT.Sqrt)
 
         acc = [acc_pool.tile([P, L2], F32, name="acc%d" % rt) for rt in range(ROW_TILES)]
+        h = [norm_pool.tile([P, L1], BF16, name="h%d" % rt) for rt in range(ROW_TILES)]
+        sums = [norm_pool.tile([P, QUARTERS], F32, name="sums%d" % rt) for rt in range(ROW_TILES)]
+        squares = [norm_pool.tile([P, QUARTERS], F32, name="squares%d" % rt) for rt in range(ROW_TILES)]
+        neg_mean = [norm_pool.tile([P, 1], F32, name="neg_mean%d" % rt) for rt in range(ROW_TILES)]
+        rstd = [norm_pool.tile([P, 1], F32, name="rstd%d" % rt) for rt in range(ROW_TILES)]
 
         def load_chunk(src, rt, col0):
             raw = raw_pool.tile([P, CHUNK], BF16, tag="raw")
             nc.sync.dma_start(out=raw[:], in_=src[rt * P : (rt + 1) * P, col0 : col0 + CHUNK])
             return raw
 
-        def prepare_pass(rows, word0, kind, copies):
-            grouped = group_pool.tile([P, B * PACK], BF16, align_bytes=64, tag="grouped_" + kind)
+        def load_logits(rt, j):
+            cols = slice(j * CHUNK, (j + 1) * CHUNK)
+            nc.sync.dma_start(out=h[rt][:, cols], in_=mid_logits[rt * P : (rt + 1) * P, cols])
+
+        def load_x_quarter(q):
+            w_raw = [load_chunk(W2, rt, L1 + q * CHUNK) for rt in range(ROW_TILES)]
+            load_logits(q, 0)
+            load_logits(q, 1)
+            x_raw = [load_chunk(x, rt, q * CHUNK) for rt in (0, 1)]
+            load_logits(q, 2)
+            x_raw.extend([load_chunk(x, rt, q * CHUNK) for rt in (2, 3)])
+            load_logits(q, 3)
+            return w_raw, x_raw
+
+        def load_hn_quarter(q):
+            return [load_chunk(W2, rt, q * CHUNK) for rt in range(ROW_TILES)]
+
+        def relu_slice(rt, j):
+            cols = slice(j * CHUNK, (j + 1) * CHUNK)
+            nc.vector.tensor_scalar(
+                out=h[rt][:, cols], in0=h[rt][:, cols], scalar1=0.0, scalar2=None,
+                op0=ALU.max, op1=ALU.add, accum_out=sums[rt][:, j : j + 1],
+            )
+            if j == QUARTERS - 1:
+                total = norm_pool.tile([P, 1], F32, name="total%d" % rt)
+                nc.vector.tensor_reduce(out=total[:], in_=sums[rt][:], axis=AX.X, op=ALU.add)
+                nc.vector.tensor_scalar_mul(out=neg_mean[rt][:], in0=total[:], scalar1=-1.0 / L1)
+
+        def square_slice(rt, j):
+            cols = slice(j * CHUNK, (j + 1) * CHUNK)
+            scrap = scrap_pool.tile([P, CHUNK], BF16)
+            nc.scalar.activation(
+                out=scrap[:], in_=h[rt][:, cols], func=ACT.Square, bias=neg_mean[rt][:, 0:1], scale=1.0,
+                accum_out=squares[rt][:, j : j + 1],
+            )
+
+        def deviation(rt):
+            spread = norm_pool.tile([P, 1], F32, name="spread%d" % rt)
+            nc.vector.tensor_reduce(out=spread[:], in_=squares[rt][:], axis=AX.X, op=ALU.add)
+            std = norm_pool.tile([P, 1], F32, name="std%d" % rt)
+            nc.scalar.activation(out=std[:], in_=spread[:], func=ACT.Sqrt, bias=LN_EPS, scale=1.0 / L1)
+            return std
+
+        def scale_slice(rt, j):
+            cols = slice(j * CHUNK, (j + 1) * CHUNK)
+            nc.vector.tensor_scalar(
+                out=h[rt][:, cols], in0=h[rt][:, cols], scalar1=neg_mean[rt][:, 0:1], scalar2=rstd[rt][:, 0:1],
+                op0=ALU.add, op1=ALU.mult,
+            )
+
+        waiting = []
+
+        def block(rows, g):
+            return rows[:].bitcast(F32)[:, g * WORDS_PASS : (g + 1) * WORDS_PASS]
+
+        def multiply(rt, r_mx, r_col, w_mx, w_col, first, last):
+            nc.tensor.matmul_mx(
+                out=acc[rt][:],
+                lhsT=r_mx[0][:, r_col : r_col + P].bitcast(FP8X4),
+                lhsT_scale=r_mx[1][:, r_col : r_col + P],
+                rhs=w_mx[0][:, w_col : w_col + L2].bitcast(FP8X4),
+                rhs_scale=w_mx[1][:, w_col : w_col + L2],
+                start=first,
+                stop=last,
+            )
+
+        def step(s, blocks, pool):
+            relu_t = s - RELU_STEP0
+            square_t = s - SQUARE_STEP0
+            scale_t = s - SCALE_STEP0
+            squaring = 0 <= square_t < NORM_SLICES
+            scaling = 0 <= scale_t < NORM_SLICES
+            vector_banks = 2 if squaring else 1
+            grouped = group_pool.tile([P, BLOCKS_STEP * P * PACK], BF16, align_bytes=64)
             grouped_words = grouped[:].bitcast(F32)
-            for pair in range(2):
-                bank = bank_pool.tile([P, 2, 2, P], F32, tag="bank")
+            bank_words = 2 * 2 * P
+            for t in range(BANKS_STEP):
+                bank = bank_pool.tile([P, 2, 2, P], F32)
                 for a in range(2):
-                    words = rows[2 * pair + a][:].bitcast(F32)
                     for u in range(2):
-                        first = word0 + u * P
-                        nc.tensor.transpose(bank[:, a, u, :], words[:, first : first + P], ident[:])
-                copies[pair](
-                    out=grouped_words[:, pair * 2 * 2 * P : (pair + 1) * 2 * 2 * P].rearrange(
+                        nc.tensor.transpose(bank[:, a, u, :], blocks[2 * t + a][:, u * P : (u + 1) * P], ident[:])
+                copy = nc.vector.tensor_copy if t >= BANKS_STEP - vector_banks else nc.scalar.copy
+                copy(
+                    out=grouped_words[:, t * bank_words : (t + 1) * bank_words].rearrange(
                         "p (a r u) -> p a r u", a=2, u=2
                     ),
                     in_=bank[:].rearrange("p a u r -> p a r u"),
                 )
-            codes = code_pool.tile([P, B], U32, align_bytes=64, tag="codes_" + kind)
-            scales = code_pool.tile([P, B], U8, align_bytes=64, tag="scales_" + kind)
+            for product in waiting:
+                multiply(*product)
+            waiting[:] = []
+            std = None
+            if scaling and scale_t % QUARTERS == 0:
+                std = deviation(scale_t // QUARTERS)
+            if 0 <= relu_t < NORM_SLICES:
+                relu_slice(relu_t // QUARTERS, relu_t % QUARTERS)
+            if squaring:
+                square_slice(square_t // QUARTERS, square_t % QUARTERS)
+            codes = pool.tile([P, BLOCKS_STEP * P], U32, align_bytes=64)
+            scales = pool.tile([P, BLOCKS_STEP * P], U8, align_bytes=64)
             nc.vector.quantize_mx(out=codes[:].bitcast(FP8X4), scales=scales[:], in_=grouped[:])
+            if std is not None:
+                nc.vector.reciprocal(out=rstd[scale_t // QUARTERS][:], in_=std[:])
+            if scaling:
+                scale_slice(scale_t // QUARTERS, scale_t % QUARTERS)
             return codes, scales
 
-        def multiply_pass(c_mx, w_mx, first, last):
-            c_codes, c_scales = c_mx
-            w_codes, w_scales = w_mx
-            for rt in range(ROW_TILES):
-                cols = slice(rt * P, (rt + 1) * P)
-                nc.tensor.matmul_mx(
-                    out=acc[rt][:],
-                    lhsT=c_codes[:, cols].bitcast(FP8X4),
-                    lhsT_scale=c_scales[:, cols],
-                    rhs=w_codes[:].bitcast(FP8X4),
-                    rhs_scale=w_scales[:],
-                    start=first,
-                    stop=last,
-                )
+        def weight_blocks(w_raw, passes):
+            return [block(w_raw[rt], j) for j in passes for rt in range(ROW_TILES)]
 
-        def normalise(h):
-            sums = stat_pool.tile([P, L1 // CHUNK], F32)
-            for j in range(L1 // CHUNK):
-                cols = slice(j * CHUNK, (j + 1) * CHUNK)
-                nc.vector.tensor_scalar(
-                    out=h[:, cols], in0=h[:, cols], scalar1=0.0, scalar2=None,
-                    op0=ALU.max, op1=ALU.add, accum_out=sums[:, j : j + 1],
-                )
-            total = stat_pool.tile([P, 1], F32)
-            nc.vector.tensor_reduce(out=total[:], in_=sums[:], axis=AX.X, op=ALU.add)
-            neg_mean = stat_pool.tile([P, 1], F32)
-            nc.vector.tensor_scalar_mul(out=neg_mean[:], in0=total[:], scalar1=-1.0 / L1)
-            squares = stat_pool.tile([P, L1 // CHUNK], F32)
-            for j in range(L1 // CHUNK):
-                cols = slice(j * CHUNK, (j + 1) * CHUNK)
-                scrap = scrap_pool.tile([P, CHUNK], BF16)
-                nc.scalar.activation(
-                    out=scrap[:], in_=h[:, cols], func=ACT.Square, bias=neg_mean[:, 0:1], scale=1.0,
-                    accum_out=squares[:, j : j + 1],
-                )
-            spread = stat_pool.tile([P, 1], F32)
-            nc.vector.tensor_reduce(out=spread[:], in_=squares[:], axis=AX.X, op=ALU.add)
-            std = stat_pool.tile([P, 1], F32)
-            nc.scalar.activation(out=std[:], in_=spread[:], func=ACT.Sqrt, bias=LN_EPS, scale=1.0 / L1)
-            rstd = stat_pool.tile([P, 1], F32)
-            nc.vector.reciprocal(out=rstd[:], in_=std[:])
-            for j in range(L1 // CHUNK):
-                cols = slice(j * CHUNK, (j + 1) * CHUNK)
-                nc.vector.tensor_scalar(
-                    out=h[:, cols], in0=h[:, cols], scalar1=neg_mean[:, 0:1], scalar2=rstd[:, 0:1],
-                    op0=ALU.add, op1=ALU.mult,
-                )
+        def rows_blocks(tiles, pair, g0):
+            return [block(tiles[2 * pair + a], g0 + j) for j in range(PASSES_CHUNK) for a in range(2)]
 
-        to_scalar = nc.scalar.copy
-        to_vector = nc.vector.tensor_copy
+        def queue_products(pair, r_mx, w_mx, first, last):
+            for a in range(2):
+                for j in range(PASSES_CHUNK):
+                    waiting.append(
+                        (2 * pair + a, r_mx, (2 * j + a) * P, w_mx[j // 2], (j % 2) * L2,
+                         first and j == 0, last and j == PASSES_CHUNK - 1)
+                    )
 
-        hn = []
-        for q in range(D // CHUNK):
-            w_rows = [load_chunk(W2, rt, L1 + q * CHUNK) for rt in range(ROW_TILES)]
-            x_rows = [load_chunk(x, rt, q * CHUNK) for rt in range(ROW_TILES)]
-            h = norm_pool.tile([P, L1], BF16, name="h%d" % q)
-            for j in range(L1 // CHUNK):
-                cols = slice(j * CHUNK, (j + 1) * CHUNK)
-                nc.sync.dma_start(out=h[:, cols], in_=mid_logits[q * P : (q + 1) * P, cols])
-            hn.append(h)
-            for j in range(PASSES_CHUNK):
-                w_mx = prepare_pass(w_rows, j * WORDS_PASS, "w", (to_scalar, to_scalar))
-                c_mx = prepare_pass(x_rows, j * WORDS_PASS, "c", (to_scalar, to_vector))
-                multiply_pass(c_mx, w_mx, q == 0 and j == 0, False)
-            normalise(h)
-
+        x_loads = [load_x_quarter(0), load_x_quarter(1)]
+        hn_loads = []
+        s = 0
+        for q in range(QUARTERS):
+            w_raw, x_raw = x_loads[q]
+            w_mx = []
+            for passes in ((0, 1), (2, 3)):
+                w_mx.append(step(s, weight_blocks(w_raw, passes), weight_pool))
+                s += 1
+            for pair in range(2):
+                r_mx = step(s, rows_blocks(x_raw, pair, 0), rows_pool)
+                s += 1
+                queue_products(pair, r_mx, w_mx, q == 0, False)
+            if q + 2 < QUARTERS:
+                x_loads.append(load_x_quarter(q + 2))
+            else:
+                hn_loads.append(load_hn_quarter(2 * (q + 2 - QUARTERS)))
+                hn_loads.append(load_hn_quarter(2 * (q + 2 - QUARTERS) + 1))
         bias = tail_pool.tile([P, L2], BF16)
         nc.sync.dma_start(out=bias[:], in_=b2.partition_broadcast(P))
 
-        for q in range(L1 // CHUNK):
-            w_rows = [load_chunk(W2, rt, q * CHUNK) for rt in range(ROW_TILES)]
-            for j in range(PASSES_CHUNK):
-                g = q * PASSES_CHUNK + j
-                w_mx = prepare_pass(w_rows, j * WORDS_PASS, "w", (to_scalar, to_scalar))
-                c_mx = prepare_pass(hn, g * WORDS_PASS, "c", (to_scalar, to_vector))
-                multiply_pass(c_mx, w_mx, False, g == L1 // K_PASS - 1)
+        hn_w_mx = []
+        for q in range(QUARTERS):
+            w_mx = []
+            for passes in ((0, 1), (2, 3)):
+                w_mx.append(step(s, weight_blocks(hn_loads[q], passes), weight_pool))
+                s += 1
+            hn_w_mx.append(w_mx)
+            r_mx = step(s, rows_blocks(h, 0, q * PASSES_CHUNK), rows_pool)
+            s += 1
+            queue_products(0, r_mx, w_mx, False, q == QUARTERS - 1)
 
         exp_sums = tail_pool.tile([P, ROW_TILES], F32)
-        logits = []
-        neg_maxes = []
-        for rt in range(ROW_TILES):
-            li = tail_pool.tile([P, L2], F32, name="li%d" % rt)
-            nc.vector.tensor_tensor(out=li[:], in0=acc[rt][:], in1=bias[:], op=ALU.add)
+        li = [tail_pool.tile([P, L2], F32, name="li%d" % rt) for rt in range(ROW_TILES)]
+        neg_max = [tail_pool.tile([P, 1], F32, name="neg_max%d" % rt) for rt in range(ROW_TILES)]
+
+        def softmax_front(rt):
+            nc.vector.tensor_tensor(out=li[rt][:], in0=acc[rt][:], in1=bias[:], op=ALU.add)
             row_max = tail_pool.tile([P, 1], F32, name="row_max%d" % rt)
-            nc.vector.reduce_max(out=row_max[:], in_=li[:], axis=AX.X)
-            neg_max = tail_pool.tile([P, 1], F32, name="neg_max%d" % rt)
-            nc.vector.tensor_scalar_mul(out=neg_max[:], in0=row_max[:], scalar1=-1.0)
-            e = tail_pool.tile([P, L2], F32, name="e%d" % rt)
+            nc.vector.reduce_max(out=row_max[:], in_=li[rt][:], axis=AX.X)
+            nc.vector.tensor_scalar_mul(out=neg_max[rt][:], in0=row_max[:], scalar1=-1.0)
+            e = scrap_pool.tile([P, L2], F32)
             nc.scalar.activation(
-                out=e[:], in_=li[:], func=ACT.Exp, bias=neg_max[:, 0:1], scale=1.0,
+                out=e[:], in_=li[rt][:], func=ACT.Exp, bias=neg_max[rt][:, 0:1], scale=1.0,
                 accum_out=exp_sums[:, rt : rt + 1],
             )
-            logits.append(li)
-            neg_maxes.append(neg_max)
+
+        for q in range(QUARTERS):
+            r_mx = step(s, rows_blocks(h, 1, q * PASSES_CHUNK), rows_pool)
+            s += 1
+            if q == 0:
+                softmax_front(0)
+                softmax_front(1)
+            queue_products(1, r_mx, hn_w_mx[q], False, q == QUARTERS - 1)
+        for product in waiting:
+            multiply(*product)
+        softmax_front(2)
+        softmax_front(3)
+
         log_sums = tail_pool.tile([P, ROW_TILES], F32)
         nc.scalar.activation(out=log_sums[:], in_=exp_sums[:], func=ACT.Ln)
         for rt in range(ROW_TILES):
-            li = logits[rt]
             nc.vector.tensor_scalar(
-                out=li[:], in0=li[:], scalar1=neg_maxes[rt][:, 0:1], scalar2=log_sums[:, rt : rt + 1],
+                out=li[rt][:], in0=li[rt][:], scalar1=neg_max[rt][:, 0:1], scalar2=log_sums[:, rt : rt + 1],
                 op0=ALU.add, op1=ALU.subtract,
             )
-            nc.sync.dma_start(out=out[rt * P : (rt + 1) * P, :], in_=li[:])
+            nc.sync.dma_start(out=out[rt * P : (rt + 1) * P, :], in_=li[rt][:])

@@ -16,7 +16,6 @@ P = 128
 PACK = 4
 K_PASS = P * PACK
 WORDS_PASS = K_PASS // 2
-
 B = 512
 L1 = 8192
 D = 8192
@@ -25,14 +24,32 @@ ROW_TILES = B // P
 CHUNK = 2048
 QUARTERS = L1 // CHUNK
 PASSES_CHUNK = CHUNK // K_PASS
+PASSES_HALF = L1 // K_PASS
+PASSES = 2 * PASSES_HALF
 BLOCKS_STEP = 8
 BANKS_STEP = 4
 LN_EPS = 1e-5
 
-RELU_STEP0 = 2
-SQUARE_STEP0 = RELU_STEP0 + QUARTERS
-SCALE_STEP0 = SQUARE_STEP0 + QUARTERS
-NORM_SLICES = ROW_TILES * QUARTERS
+PIECE = 1024
+PIECES = L1 // PIECE
+NORM_NUM = 7
+NORM_DEN = 8
+S_LAG = 0
+STATS_LAG = 1
+SCALE_LAG = 1
+SCALES_PER_STEP = 2
+LAG = 2
+RUN_EVERY = 1
+RAW_BUFS = 12
+GROUP_BUFS = 2
+WX_BUFS = 3
+XR_BUFS = 3
+HR_BUFS = 3
+MID_AHEAD = 1
+VB_DEFAULT = 1
+VB2_EVERY = 0
+VB2_AFTER = 99
+NONH_ORDER = 0
 
 FLOPS = 2 * B * L2 * (L1 + D)
 
@@ -41,12 +58,14 @@ def tile_bhcn_awx_pa_k_kernel(tc, mid_logits, x, W2, b2, out):
     nc = tc.nc
     with ExitStack() as stack:
         const_pool = stack.enter_context(tc.tile_pool(name="const", bufs=1))
-        raw_pool = stack.enter_context(tc.tile_pool(name="raw", bufs=16))
+        raw_pool = stack.enter_context(tc.tile_pool(name="raw", bufs=RAW_BUFS))
         norm_pool = stack.enter_context(tc.tile_pool(name="norm", bufs=1))
         scrap_pool = stack.enter_context(tc.tile_pool(name="scrap", bufs=2))
-        group_pool = stack.enter_context(tc.tile_pool(name="group", bufs=2))
-        weight_pool = stack.enter_context(tc.tile_pool(name="weight", bufs=2 * QUARTERS))
-        rows_pool = stack.enter_context(tc.tile_pool(name="rows", bufs=3))
+        group_pool = stack.enter_context(tc.tile_pool(name="group", bufs=GROUP_BUFS))
+        wx_pool = stack.enter_context(tc.tile_pool(name="wx", bufs=WX_BUFS))
+        wh_pool = stack.enter_context(tc.tile_pool(name="wh", bufs=PASSES_HALF // 2))
+        xr_pool = stack.enter_context(tc.tile_pool(name="xr", bufs=XR_BUFS))
+        hr_pool = stack.enter_context(tc.tile_pool(name="hr", bufs=HR_BUFS))
         tail_pool = stack.enter_context(tc.tile_pool(name="tail", bufs=1))
         acc_pool = stack.enter_context(tc.psum_pool(name="acc", bufs=1))
         bank_pool = stack.enter_context(tc.psum_pool(name="bank", bufs=BANKS_STEP))
@@ -61,94 +80,230 @@ def tile_bhcn_awx_pa_k_kernel(tc, mid_logits, x, W2, b2, out):
 
         acc = [acc_pool.tile([P, L2], F32, name="acc%d" % rt) for rt in range(ROW_TILES)]
         h = [norm_pool.tile([P, L1], BF16, name="h%d" % rt) for rt in range(ROW_TILES)]
-        sums = [norm_pool.tile([P, QUARTERS], F32, name="sums%d" % rt) for rt in range(ROW_TILES)]
-        squares = [norm_pool.tile([P, QUARTERS], F32, name="squares%d" % rt) for rt in range(ROW_TILES)]
+        sums = [norm_pool.tile([P, PIECES], F32, name="sums%d" % rt) for rt in range(ROW_TILES)]
+        squares = [norm_pool.tile([P, PIECES], F32, name="squares%d" % rt) for rt in range(ROW_TILES)]
+        neg_shift = [norm_pool.tile([P, 1], F32, name="neg_shift%d" % rt) for rt in range(ROW_TILES)]
         neg_mean = [norm_pool.tile([P, 1], F32, name="neg_mean%d" % rt) for rt in range(ROW_TILES)]
+        total = [norm_pool.tile([P, 1], F32, name="total%d" % rt) for rt in range(ROW_TILES)]
+        gap2 = [norm_pool.tile([P, 1], F32, name="gap2%d" % rt) for rt in range(ROW_TILES)]
+        spread = [norm_pool.tile([P, 1], F32, name="spread%d" % rt) for rt in range(ROW_TILES)]
+        var = [norm_pool.tile([P, 1], F32, name="var%d" % rt) for rt in range(ROW_TILES)]
+        std = [norm_pool.tile([P, 1], F32, name="std%d" % rt) for rt in range(ROW_TILES)]
         rstd = [norm_pool.tile([P, 1], F32, name="rstd%d" % rt) for rt in range(ROW_TILES)]
 
-        def load_chunk(src, rt, col0):
-            raw = raw_pool.tile([P, CHUNK], BF16, tag="raw")
-            nc.sync.dma_start(out=raw[:], in_=src[rt * P : (rt + 1) * P, col0 : col0 + CHUNK])
-            return raw
+        n_steps = 32
+        relu_at = {}
+        square_at = {}
+        stats_at = {}
+        scale_at = {}
+        h_ready = {}
+        for i in range(ROW_TILES * PIECES):
+            s = (i * NORM_NUM) // NORM_DEN
+            relu_at.setdefault(s, []).append(i)
+            square_at.setdefault(s + S_LAG, []).append(i)
+        for rt in range(ROW_TILES):
+            a = ((rt * PIECES + PIECES - 1) * NORM_NUM) // NORM_DEN + S_LAG
+            stats_at[a + STATS_LAG] = rt
+            for j in range(QUARTERS):
+                s = a + STATS_LAG + SCALE_LAG + j // SCALES_PER_STEP
+                scale_at.setdefault(s, []).append((rt, j))
+                if j % 2 == 1:
+                    h_ready[(rt, j // 2)] = s + 1
+        if NONH_ORDER == 0:
+            non_h = []
+            for q in range(QUARTERS):
+                for pp in range(2):
+                    non_h.append(("W", PASSES_HALF + q * PASSES_CHUNK + 2 * pp))
+                    non_h.append(("X", PASSES_HALF + q * PASSES_CHUNK + 2 * pp))
+                if q < 2:
+                    for qq in (2 * q, 2 * q + 1):
+                        for pp in range(2):
+                            non_h.append(("W", qq * PASSES_CHUNK + 2 * pp))
+        elif NONH_ORDER == 1:
+            non_h = []
+            for q in range(QUARTERS):
+                for pp in range(2):
+                    non_h.append(("W", PASSES_HALF + q * PASSES_CHUNK + 2 * pp))
+                    non_h.append(("X", PASSES_HALF + q * PASSES_CHUNK + 2 * pp))
+                for pp in range(2):
+                    non_h.append(("W", q * PASSES_CHUNK + 2 * pp))
+        else:
+            non_h = []
+            for q in range(QUARTERS):
+                for pp in range(2):
+                    non_h.append(("W", q * PASSES_CHUNK + 2 * pp))
+                for pp in range(2):
+                    non_h.append(("W", PASSES_HALF + q * PASSES_CHUNK + 2 * pp))
+                    non_h.append(("X", PASSES_HALF + q * PASSES_CHUNK + 2 * pp))
+        h_steps = [(rt, part) for rt in range(ROW_TILES) for part in range(2)]
+        order = []
+        taken_h = 0
+        for s in range(n_steps):
+            if taken_h < len(h_steps) and (h_ready[h_steps[taken_h]] <= s or s - taken_h >= len(non_h)):
+                order.append(("H",) + h_steps[taken_h])
+                taken_h += 1
+            else:
+                order.append(non_h[s - taken_h])
 
-        def load_logits(rt, j):
-            cols = slice(j * CHUNK, (j + 1) * CHUNK)
-            nc.sync.dma_start(out=h[rt][:, cols], in_=mid_logits[rt * P : (rt + 1) * P, cols])
+        raw = {}
+        fifo = []
+        seen = set()
+        for s, what in enumerate(order):
+            for i in relu_at.get(s + MID_AHEAD, []) + (relu_at.get(s, []) if s == 0 else []):
+                key = ("M", i // PIECES, (i % PIECES) * PIECE // CHUNK)
+                if key not in seen:
+                    seen.add(key)
+                    fifo.append(key)
+            if what[0] != "H":
+                key = (what[0], what[1] // PASSES_CHUNK)
+                if key not in seen:
+                    seen.add(key)
+                    for rt in range(ROW_TILES):
+                        fifo.append(key + (rt,))
+        for i in range(ROW_TILES * PIECES):
+            key = ("M", i // PIECES, (i % PIECES) * PIECE // CHUNK)
+            if key not in seen:
+                seen.add(key)
+                fifo.append(key)
+        live = [0]
+        loaded = [0]
 
-        def load_x_quarter(q):
-            w_raw = [load_chunk(W2, rt, L1 + q * CHUNK) for rt in range(ROW_TILES)]
-            load_logits(q, 0)
-            load_logits(q, 1)
-            x_raw = [load_chunk(x, rt, q * CHUNK) for rt in (0, 1)]
-            load_logits(q, 2)
-            x_raw.extend([load_chunk(x, rt, q * CHUNK) for rt in (2, 3)])
-            load_logits(q, 3)
-            return w_raw, x_raw
+        def pump():
+            while loaded[0] < len(fifo):
+                key = fifo[loaded[0]]
+                if key[0] == "M":
+                    cols = slice(key[2] * CHUNK, (key[2] + 1) * CHUNK)
+                    nc.sync.dma_start(out=h[key[1]][:, cols], in_=mid_logits[key[1] * P : (key[1] + 1) * P, cols])
+                else:
+                    if live[0] >= RAW_BUFS:
+                        return
+                    live[0] += 1
+                    chunk = raw_pool.tile([P, CHUNK], BF16, tag="raw")
+                    src = W2 if key[0] == "W" else x
+                    col0 = key[1] * CHUNK if key[0] == "W" else (key[1] - QUARTERS) * CHUNK
+                    nc.sync.dma_start(out=chunk[:], in_=src[key[2] * P : (key[2] + 1) * P, col0 : col0 + CHUNK])
+                    raw[key] = chunk
+                loaded[0] += 1
 
-        def load_hn_quarter(q):
-            return [load_chunk(W2, rt, q * CHUNK) for rt in range(ROW_TILES)]
-
-        def relu_slice(rt, j):
-            cols = slice(j * CHUNK, (j + 1) * CHUNK)
+        def relu_piece(i):
+            rt, j = i // PIECES, i % PIECES
+            cols = slice(j * PIECE, (j + 1) * PIECE)
             nc.vector.tensor_scalar(
                 out=h[rt][:, cols], in0=h[rt][:, cols], scalar1=0.0, scalar2=None,
                 op0=ALU.max, op1=ALU.add, accum_out=sums[rt][:, j : j + 1],
             )
-            if j == QUARTERS - 1:
-                total = norm_pool.tile([P, 1], F32, name="total%d" % rt)
-                nc.vector.tensor_reduce(out=total[:], in_=sums[rt][:], axis=AX.X, op=ALU.add)
-                nc.vector.tensor_scalar_mul(out=neg_mean[rt][:], in0=total[:], scalar1=-1.0 / L1)
+            if j == 0:
+                nc.vector.tensor_scalar_mul(out=neg_shift[rt][:], in0=sums[rt][:, 0:1], scalar1=-1.0 / PIECE)
+            if j == PIECES - 1:
+                nc.vector.tensor_reduce(out=total[rt][:], in_=sums[rt][:], axis=AX.X, op=ALU.add)
+                nc.vector.tensor_scalar_mul(out=neg_mean[rt][:], in0=total[rt][:], scalar1=-1.0 / L1)
 
-        def square_slice(rt, j):
-            cols = slice(j * CHUNK, (j + 1) * CHUNK)
-            scrap = scrap_pool.tile([P, CHUNK], BF16)
+        def square_piece(i):
+            rt, j = i // PIECES, i % PIECES
+            cols = slice(j * PIECE, (j + 1) * PIECE)
+            scrap = scrap_pool.tile([P, PIECE], BF16, tag="scrap")
             nc.scalar.activation(
-                out=scrap[:], in_=h[rt][:, cols], func=ACT.Square, bias=neg_mean[rt][:, 0:1], scale=1.0,
+                out=scrap[:], in_=h[rt][:, cols], func=ACT.Square, bias=neg_shift[rt][:, 0:1], scale=1.0,
                 accum_out=squares[rt][:, j : j + 1],
             )
+            if j == PIECES - 1:
+                nc.scalar.activation(out=gap2[rt][:], in_=total[rt][:], func=ACT.Square, bias=neg_shift[rt][:, 0:1], scale=1.0 / L1)
 
-        def deviation(rt):
-            spread = norm_pool.tile([P, 1], F32, name="spread%d" % rt)
-            nc.vector.tensor_reduce(out=spread[:], in_=squares[rt][:], axis=AX.X, op=ALU.add)
-            std = norm_pool.tile([P, 1], F32, name="std%d" % rt)
-            nc.scalar.activation(out=std[:], in_=spread[:], func=ACT.Sqrt, bias=LN_EPS, scale=1.0 / L1)
-            return std
+        def stats_vector(rt):
+            nc.vector.tensor_reduce(out=spread[rt][:], in_=squares[rt][:], axis=AX.X, op=ALU.add)
+            nc.vector.scalar_tensor_tensor(
+                out=var[rt][:], in0=spread[rt][:], scalar=1.0 / L1, in1=gap2[rt][:], op0=ALU.mult, op1=ALU.subtract
+            )
+
+        def stats_scalar(rt):
+            nc.scalar.activation(out=std[rt][:], in_=var[rt][:], func=ACT.Sqrt, bias=LN_EPS, scale=1.0)
 
         def scale_slice(rt, j):
+            if j == 0:
+                nc.vector.reciprocal(out=rstd[rt][:], in_=std[rt][:])
             cols = slice(j * CHUNK, (j + 1) * CHUNK)
             nc.vector.tensor_scalar(
                 out=h[rt][:, cols], in0=h[rt][:, cols], scalar1=neg_mean[rt][:, 0:1], scalar2=rstd[rt][:, 0:1],
                 op0=ALU.add, op1=ALU.mult,
             )
 
-        waiting = []
+        w_codes = {}
+        r_codes = {}
+        ready = []
+        issued = [0] * ROW_TILES
+        closed = []
 
-        def block(rows, g):
-            return rows[:].bitcast(F32)[:, g * WORDS_PASS : (g + 1) * WORDS_PASS]
-
-        def multiply(rt, r_mx, r_col, w_mx, w_col, first, last):
+        def multiply(rt, g):
+            r_mx, r_col = r_codes[(rt, g)]
+            w_mx, w_col = w_codes[g]
             nc.tensor.matmul_mx(
                 out=acc[rt][:],
                 lhsT=r_mx[0][:, r_col : r_col + P].bitcast(FP8X4),
                 lhsT_scale=r_mx[1][:, r_col : r_col + P],
                 rhs=w_mx[0][:, w_col : w_col + L2].bitcast(FP8X4),
                 rhs_scale=w_mx[1][:, w_col : w_col + L2],
-                start=first,
-                stop=last,
+                start=issued[rt] == 0,
+                stop=issued[rt] == PASSES - 1,
+            )
+            issued[rt] += 1
+            if issued[rt] == PASSES:
+                closed.append(rt)
+
+        done = [0]
+
+        def run_products(s):
+            while done[0] < len(ready) and ready[done[0]][0] <= s - LAG:
+                multiply(*ready[done[0]][1:])
+                done[0] += 1
+
+        bias = tail_pool.tile([P, L2], BF16)
+        exp_sums = tail_pool.tile([P, ROW_TILES], F32)
+        li = [tail_pool.tile([P, L2], F32, name="li%d" % rt) for rt in range(ROW_TILES)]
+        neg_max = [tail_pool.tile([P, 1], F32, name="neg_max%d" % rt) for rt in range(ROW_TILES)]
+
+        def softmax_front(rt):
+            nc.vector.tensor_tensor(out=li[rt][:], in0=acc[rt][:], in1=bias[:], op=ALU.add)
+            row_max = tail_pool.tile([P, 1], F32, name="row_max%d" % rt)
+            nc.vector.reduce_max(out=row_max[:], in_=li[rt][:], axis=AX.X)
+            nc.vector.tensor_scalar_mul(out=neg_max[rt][:], in0=row_max[:], scalar1=-1.0)
+            e = scrap_pool.tile([P, L2], F32, tag="scrap")
+            nc.scalar.activation(
+                out=e[:], in_=li[rt][:], func=ACT.Exp, bias=neg_max[rt][:, 0:1], scale=1.0,
+                accum_out=exp_sums[:, rt : rt + 1],
             )
 
-        def step(s, blocks, pool):
-            relu_t = s - RELU_STEP0
-            square_t = s - SQUARE_STEP0
-            scale_t = s - SCALE_STEP0
-            squaring = 0 <= square_t < NORM_SLICES
-            scaling = 0 <= scale_t < NORM_SLICES
-            vector_banks = 2 if squaring else 1
-            grouped = group_pool.tile([P, BLOCKS_STEP * P * PACK], BF16, align_bytes=64)
+        def block(rows, g):
+            return rows[:].bitcast(F32)[:, g * WORDS_PASS : (g + 1) * WORDS_PASS]
+
+        def step(s, what):
+            if what[0] == "W":
+                g0 = what[1]
+                q = g0 // PASSES_CHUNK
+                blocks = [block(raw[("W", q, rt)], (g0 + j) % PASSES_CHUNK) for j in range(2) for rt in range(ROW_TILES)]
+                pool = wx_pool if g0 >= PASSES_HALF else wh_pool
+            elif what[0] == "X":
+                g0 = what[1]
+                q = g0 // PASSES_CHUNK
+                blocks = [block(raw[("X", q, rt)], (g0 + j) % PASSES_CHUNK) for j in range(2) for rt in range(ROW_TILES)]
+                pool = xr_pool
+            else:
+                rt, part = what[1], what[2]
+                blocks = [block(h[rt], part * BLOCKS_STEP + j) for j in range(BLOCKS_STEP)]
+                pool = hr_pool
+            for i in relu_at.get(s, []):
+                relu_piece(i)
+            late = closed[:]
+            closed[:] = []
+            vector_banks = VB_DEFAULT
+            if VB2_EVERY and s % VB2_EVERY == VB2_EVERY - 1:
+                vector_banks = 2
+            if s >= VB2_AFTER:
+                vector_banks = 2
+            grouped = group_pool.tile([P, BLOCKS_STEP * P * PACK], BF16, align_bytes=64, tag="grouped")
             grouped_words = grouped[:].bitcast(F32)
             bank_words = 2 * 2 * P
             for t in range(BANKS_STEP):
-                bank = bank_pool.tile([P, 2, 2, P], F32)
+                bank = bank_pool.tile([P, 2, 2, P], F32, tag="bank")
                 for a in range(2):
                     for u in range(2):
                         nc.tensor.transpose(bank[:, a, u, :], blocks[2 * t + a][:, u * P : (u + 1) * P], ident[:])
@@ -159,97 +314,54 @@ def tile_bhcn_awx_pa_k_kernel(tc, mid_logits, x, W2, b2, out):
                     ),
                     in_=bank[:].rearrange("p a u r -> p a r u"),
                 )
-            for product in waiting:
-                multiply(*product)
-            waiting[:] = []
-            std = None
-            if scaling and scale_t % QUARTERS == 0:
-                std = deviation(scale_t // QUARTERS)
-            if 0 <= relu_t < NORM_SLICES:
-                relu_slice(relu_t // QUARTERS, relu_t % QUARTERS)
-            if squaring:
-                square_slice(square_t // QUARTERS, square_t % QUARTERS)
-            codes = pool.tile([P, BLOCKS_STEP * P], U32, align_bytes=64)
-            scales = pool.tile([P, BLOCKS_STEP * P], U8, align_bytes=64)
+            if s % RUN_EVERY == RUN_EVERY - 1:
+                run_products(s)
+            if s in stats_at:
+                stats_vector(stats_at[s])
+            for rt_j in scale_at.get(s, []):
+                scale_slice(*rt_j)
+            for rt in late:
+                softmax_front(rt)
+            for i in square_at.get(s, []):
+                square_piece(i)
+            if s in stats_at:
+                stats_scalar(stats_at[s])
+            codes = pool.tile([P, BLOCKS_STEP * P], U32, align_bytes=64, tag="codes")
+            scales = pool.tile([P, BLOCKS_STEP * P], U8, align_bytes=64, tag="scales")
             nc.vector.quantize_mx(out=codes[:].bitcast(FP8X4), scales=scales[:], in_=grouped[:])
-            if std is not None:
-                nc.vector.reciprocal(out=rstd[scale_t // QUARTERS][:], in_=std[:])
-            if scaling:
-                scale_slice(scale_t // QUARTERS, scale_t % QUARTERS)
-            return codes, scales
-
-        def weight_blocks(w_raw, passes):
-            return [block(w_raw[rt], j) for j in passes for rt in range(ROW_TILES)]
-
-        def rows_blocks(tiles, pair, g0):
-            return [block(tiles[2 * pair + a], g0 + j) for j in range(PASSES_CHUNK) for a in range(2)]
-
-        def queue_products(pair, r_mx, w_mx, first, last):
-            for a in range(2):
-                for j in range(PASSES_CHUNK):
-                    waiting.append(
-                        (2 * pair + a, r_mx, (2 * j + a) * P, w_mx[j // 2], (j % 2) * L2,
-                         first and j == 0, last and j == PASSES_CHUNK - 1)
-                    )
-
-        x_loads = [load_x_quarter(0), load_x_quarter(1)]
-        hn_loads = []
-        s = 0
-        for q in range(QUARTERS):
-            w_raw, x_raw = x_loads[q]
-            w_mx = []
-            for passes in ((0, 1), (2, 3)):
-                w_mx.append(step(s, weight_blocks(w_raw, passes), weight_pool))
-                s += 1
-            for pair in range(2):
-                r_mx = step(s, rows_blocks(x_raw, pair, 0), rows_pool)
-                s += 1
-                queue_products(pair, r_mx, w_mx, q == 0, False)
-            if q + 2 < QUARTERS:
-                x_loads.append(load_x_quarter(q + 2))
+            mx = (codes, scales)
+            if what[0] == "W":
+                for j in range(2):
+                    w_codes[g0 + j] = (mx, j * L2)
+                    for rt in range(ROW_TILES):
+                        if (rt, g0 + j) in r_codes:
+                            ready.append((s, rt, g0 + j))
+            elif what[0] == "X":
+                for j in range(2):
+                    for rt in range(ROW_TILES):
+                        r_codes[(rt, g0 + j)] = (mx, (j * ROW_TILES + rt) * P)
+                for rt in range(ROW_TILES):
+                    for j in range(2):
+                        if g0 + j in w_codes:
+                            ready.append((s, rt, g0 + j))
             else:
-                hn_loads.append(load_hn_quarter(2 * (q + 2 - QUARTERS)))
-                hn_loads.append(load_hn_quarter(2 * (q + 2 - QUARTERS) + 1))
-        bias = tail_pool.tile([P, L2], BF16)
-        nc.sync.dma_start(out=bias[:], in_=b2.partition_broadcast(P))
+                for j in range(BLOCKS_STEP):
+                    g = part * BLOCKS_STEP + j
+                    r_codes[(rt, g)] = (mx, j * P)
+                    if g in w_codes:
+                        ready.append((s, rt, g))
+            if what[0] != "H" and (what[1] % PASSES_CHUNK) == 2:
+                live[0] -= ROW_TILES
 
-        hn_w_mx = []
-        for q in range(QUARTERS):
-            w_mx = []
-            for passes in ((0, 1), (2, 3)):
-                w_mx.append(step(s, weight_blocks(hn_loads[q], passes), weight_pool))
-                s += 1
-            hn_w_mx.append(w_mx)
-            r_mx = step(s, rows_blocks(h, 0, q * PASSES_CHUNK), rows_pool)
-            s += 1
-            queue_products(0, r_mx, w_mx, False, q == QUARTERS - 1)
-
-        exp_sums = tail_pool.tile([P, ROW_TILES], F32)
-        li = [tail_pool.tile([P, L2], F32, name="li%d" % rt) for rt in range(ROW_TILES)]
-        neg_max = [tail_pool.tile([P, 1], F32, name="neg_max%d" % rt) for rt in range(ROW_TILES)]
-
-        def softmax_front(rt):
-            nc.vector.tensor_tensor(out=li[rt][:], in0=acc[rt][:], in1=bias[:], op=ALU.add)
-            row_max = tail_pool.tile([P, 1], F32, name="row_max%d" % rt)
-            nc.vector.reduce_max(out=row_max[:], in_=li[rt][:], axis=AX.X)
-            nc.vector.tensor_scalar_mul(out=neg_max[rt][:], in0=row_max[:], scalar1=-1.0)
-            e = scrap_pool.tile([P, L2], F32)
-            nc.scalar.activation(
-                out=e[:], in_=li[rt][:], func=ACT.Exp, bias=neg_max[rt][:, 0:1], scale=1.0,
-                accum_out=exp_sums[:, rt : rt + 1],
-            )
-
-        for q in range(QUARTERS):
-            r_mx = step(s, rows_blocks(h, 1, q * PASSES_CHUNK), rows_pool)
-            s += 1
-            if q == 0:
-                softmax_front(0)
-                softmax_front(1)
-            queue_products(1, r_mx, hn_w_mx[q], False, q == QUARTERS - 1)
-        for product in waiting:
-            multiply(*product)
-        softmax_front(2)
-        softmax_front(3)
+        pump()
+        for s, what in enumerate(order):
+            if s == 8:
+                nc.sync.dma_start(out=bias[:], in_=b2.partition_broadcast(P))
+            step(s, what)
+            pump()
+        run_products(n_steps + LAG)
+        for rt in closed:
+            softmax_front(rt)
 
         log_sums = tail_pool.tile([P, ROW_TILES], F32)
         nc.scalar.activation(out=log_sums[:], in_=exp_sums[:], func=ACT.Ln)

@@ -27,35 +27,42 @@ PASSES_CHUNK = CHUNK // K_PASS
 PASSES_HALF = L1 // K_PASS
 PASSES = 2 * PASSES_HALF
 BLOCKS_STEP = 8
-BANKS_STEP = 4
 LN_EPS = 1e-5
 
 PIECE = 1024
-PIECES = L1 // PIECE
 NORM_NUM = 7
 NORM_DEN = 8
-S_LAG = 0
-STATS_LAG = 1
-SCALE_LAG = 1
-SCALES_PER_STEP = 2
-LAG = 2
-RUN_EVERY = 1
+R_OFF = 1
+HEAD_DOUBLE = 0
+S_LAG = 1
+SPREAD_TINY = 1
+SCALE_PER_STEP = 1
+FAST_FROM = 3
+RIPE_FAST = 2
+LAG = 1
+RUN_MAX = 5
+TAIL_STEPS = 4
 RAW_BUFS = 12
 GROUP_BUFS = 2
 WX_BUFS = 3
 XR_BUFS = 3
 HR_BUFS = 3
 MID_AHEAD = 1
-VB_DEFAULT = 1
-VB2_EVERY = 0
-VB2_AFTER = 99
-NONH_ORDER = 0
+NARROW = 2
+SPLIT_LAST = 1
+ORDER_KIND = 0
+VB0_FROM = 99
+VB2_LIST = ()
+WARM_EXP_AT = 29
+LN_FIRST = 0
+SPLIT_FINAL = 0
 
 FLOPS = 2 * B * L2 * (L1 + D)
 
 
 def tile_bhcn_awx_pa_k_kernel(tc, mid_logits, x, W2, b2, out):
     nc = tc.nc
+    pieces = L1 // PIECE
     with ExitStack() as stack:
         const_pool = stack.enter_context(tc.tile_pool(name="const", bufs=1))
         raw_pool = stack.enter_context(tc.tile_pool(name="raw", bufs=RAW_BUFS))
@@ -68,7 +75,7 @@ def tile_bhcn_awx_pa_k_kernel(tc, mid_logits, x, W2, b2, out):
         hr_pool = stack.enter_context(tc.tile_pool(name="hr", bufs=HR_BUFS))
         tail_pool = stack.enter_context(tc.tile_pool(name="tail", bufs=1))
         acc_pool = stack.enter_context(tc.psum_pool(name="acc", bufs=1))
-        bank_pool = stack.enter_context(tc.psum_pool(name="bank", bufs=BANKS_STEP))
+        bank_pool = stack.enter_context(tc.psum_pool(name="bank", bufs=4))
         stack.enter_context(tc.manual_schedule())
 
         ident = const_pool.tile([P, P], F32)
@@ -80,8 +87,8 @@ def tile_bhcn_awx_pa_k_kernel(tc, mid_logits, x, W2, b2, out):
 
         acc = [acc_pool.tile([P, L2], F32, name="acc%d" % rt) for rt in range(ROW_TILES)]
         h = [norm_pool.tile([P, L1], BF16, name="h%d" % rt) for rt in range(ROW_TILES)]
-        sums = [norm_pool.tile([P, PIECES], F32, name="sums%d" % rt) for rt in range(ROW_TILES)]
-        squares = [norm_pool.tile([P, PIECES], F32, name="squares%d" % rt) for rt in range(ROW_TILES)]
+        sums = [norm_pool.tile([P, pieces], F32, name="sums%d" % rt) for rt in range(ROW_TILES)]
+        squares = [norm_pool.tile([P, pieces], F32, name="squares%d" % rt) for rt in range(ROW_TILES)]
         neg_shift = [norm_pool.tile([P, 1], F32, name="neg_shift%d" % rt) for rt in range(ROW_TILES)]
         neg_mean = [norm_pool.tile([P, 1], F32, name="neg_mean%d" % rt) for rt in range(ROW_TILES)]
         total = [norm_pool.tile([P, 1], F32, name="total%d" % rt) for rt in range(ROW_TILES)]
@@ -90,81 +97,205 @@ def tile_bhcn_awx_pa_k_kernel(tc, mid_logits, x, W2, b2, out):
         var = [norm_pool.tile([P, 1], F32, name="var%d" % rt) for rt in range(ROW_TILES)]
         std = [norm_pool.tile([P, 1], F32, name="std%d" % rt) for rt in range(ROW_TILES)]
         rstd = [norm_pool.tile([P, 1], F32, name="rstd%d" % rt) for rt in range(ROW_TILES)]
+        bias = tail_pool.tile([P, L2], BF16)
+        exp_sums = tail_pool.tile([P, ROW_TILES], F32)
+        li = [tail_pool.tile([P, L2], F32, name="li%d" % rt) for rt in range(ROW_TILES)]
+        neg_max = [tail_pool.tile([P, 1], F32, name="neg_max%d" % rt) for rt in range(ROW_TILES)]
 
-        n_steps = 32
-        relu_at = {}
-        square_at = {}
-        stats_at = {}
-        scale_at = {}
-        h_ready = {}
-        for i in range(ROW_TILES * PIECES):
-            s = (i * NORM_NUM) // NORM_DEN
-            relu_at.setdefault(s, []).append(i)
-            square_at.setdefault(s + S_LAG, []).append(i)
+        def relu_piece(i):
+            rt, j = i // pieces, i % pieces
+            cols = slice(j * PIECE, (j + 1) * PIECE)
+            nc.vector.tensor_scalar(
+                out=h[rt][:, cols], in0=h[rt][:, cols], scalar1=0.0, scalar2=None,
+                op0=ALU.max, op1=ALU.add, accum_out=sums[rt][:, j : j + 1],
+            )
+
+        def shift(rt):
+            nc.vector.tensor_scalar_mul(out=neg_shift[rt][:], in0=sums[rt][:, 0:1], scalar1=-1.0 / PIECE)
+
+        def row_total(rt):
+            nc.vector.tensor_reduce(out=total[rt][:], in_=sums[rt][:], axis=AX.X, op=ALU.add)
+
+        def mean(rt):
+            nc.vector.tensor_scalar_mul(out=neg_mean[rt][:], in0=total[rt][:], scalar1=-1.0 / L1)
+
+        def square_piece(i):
+            rt, j = i // pieces, i % pieces
+            cols = slice(j * PIECE, (j + 1) * PIECE)
+            scrap = scrap_pool.tile([P, PIECE], BF16, tag="scrap")
+            nc.scalar.activation(
+                out=scrap[:], in_=h[rt][:, cols], func=ACT.Square, bias=neg_shift[rt][:, 0:1], scale=1.0,
+                accum_out=squares[rt][:, j : j + 1],
+            )
+
+        def gap(rt):
+            nc.scalar.activation(out=gap2[rt][:], in_=total[rt][:], func=ACT.Square, bias=neg_shift[rt][:, 0:1], scale=1.0 / L1)
+
+        def row_spread(rt):
+            nc.vector.tensor_reduce(out=spread[rt][:], in_=squares[rt][:], axis=AX.X, op=ALU.add)
+
+        def variance(rt):
+            nc.vector.scalar_tensor_tensor(
+                out=var[rt][:], in0=spread[rt][:], scalar=1.0 / L1, in1=gap2[rt][:], op0=ALU.mult, op1=ALU.subtract
+            )
+
+        def deviation(rt):
+            nc.scalar.activation(out=std[rt][:], in_=var[rt][:], func=ACT.Sqrt, bias=LN_EPS, scale=1.0)
+
+        def inverse(rt):
+            nc.vector.reciprocal(out=rstd[rt][:], in_=std[rt][:])
+
+        def scale_slice(rt, j):
+            cols = slice(j * CHUNK, (j + 1) * CHUNK)
+            nc.vector.tensor_scalar(
+                out=h[rt][:, cols], in0=h[rt][:, cols], scalar1=neg_mean[rt][:, 0:1], scalar2=rstd[rt][:, 0:1],
+                op0=ALU.add, op1=ALU.mult,
+            )
+
+        row_max = [tail_pool.tile([P, 1], F32, name="row_max%d" % rt) for rt in range(ROW_TILES)]
+
+        def front_add(rt):
+            nc.vector.tensor_tensor(out=li[rt][:], in0=acc[rt][:], in1=bias[:], op=ALU.add)
+
+        def front_max(rt):
+            nc.vector.reduce_max(out=row_max[rt][:], in_=li[rt][:], axis=AX.X)
+
+        def front_neg(rt):
+            nc.vector.tensor_scalar_mul(out=neg_max[rt][:], in0=row_max[rt][:], scalar1=-1.0)
+
+        def front_scalar(rt):
+            e = scrap_pool.tile([P, L2], F32, tag="scrap")
+            nc.scalar.activation(
+                out=e[:], in_=li[rt][:], func=ACT.Exp, bias=neg_max[rt][:, 0:1], scale=1.0,
+                accum_out=exp_sums[:, rt : rt + 1],
+            )
+
+        def load_table(func):
+            nc.scalar.activation(out=warm[:], in_=one[:], func=func)
+
+        pre = {}
+        gapb = {}
+        mid = {}
+        post = {}
+
+        def at(where, s, fn, *args):
+            where.setdefault(s, []).append((fn, args))
+
+        def play(where, s):
+            for fn, args in where.get(s, []):
+                fn(*args)
+
+        piece_step = []
+        for i in range(ROW_TILES * pieces):
+            if i < 2 * HEAD_DOUBLE:
+                piece_step.append(R_OFF + i // 2)
+            else:
+                piece_step.append(R_OFF + HEAD_DOUBLE + ((i - 2 * HEAD_DOUBLE) * NORM_NUM) // NORM_DEN)
+        ripe = {}
+        n_pieces = ROW_TILES * pieces
+        for i, s in enumerate(piece_step):
+            rt, j = i // pieces, i % pieces
+            fast = rt >= FAST_FROM and j == pieces - 1
+            at(gapb, s, relu_piece, i)
+            at(mid, s if fast else s + S_LAG, square_piece, i)
+            if j == 0:
+                at(post, s, shift, rt)
         for rt in range(ROW_TILES):
-            a = ((rt * PIECES + PIECES - 1) * NORM_NUM) // NORM_DEN + S_LAG
-            stats_at[a + STATS_LAG] = rt
-            for j in range(QUARTERS):
-                s = a + STATS_LAG + SCALE_LAG + j // SCALES_PER_STEP
-                scale_at.setdefault(s, []).append((rt, j))
-                if j % 2 == 1:
-                    h_ready[(rt, j // 2)] = s + 1
-        if NONH_ORDER == 0:
-            non_h = []
+            a = piece_step[rt * pieces + pieces - 1]
+            if rt >= FAST_FROM:
+                at(gapb, a, row_total, rt)
+                at(mid, a, gap, rt)
+                at(post, a, mean, rt)
+                at(post, a, row_spread, rt)
+                at(post, a, variance, rt)
+                at(post, a, deviation, rt)
+                at(pre, a + 1, inverse, rt)
+                for j in range(QUARTERS):
+                    at(pre, a + 1, scale_slice, rt, j)
+                ripe[(rt, 0)] = a + RIPE_FAST
+                ripe[(rt, 1)] = a + RIPE_FAST + 1
+            else:
+                at(post, a, row_total, rt)
+                at(gapb, a + 1, mean, rt)
+                at(mid, a + S_LAG, gap, rt)
+                at(post, a + S_LAG, row_spread, rt)
+                at(gapb, a + S_LAG + 1, variance, rt)
+                at(mid, a + S_LAG + 1, deviation, rt)
+                at(post, a + S_LAG + 1, inverse, rt)
+                for j in range(QUARTERS):
+                    at(gapb, a + S_LAG + 2 + j // SCALE_PER_STEP, scale_slice, rt, j)
+                ripe[(rt, 0)] = a + S_LAG + 3 + 1 // SCALE_PER_STEP
+                ripe[(rt, 1)] = a + S_LAG + 3 + 3 // SCALE_PER_STEP
+        pairs = [[("W", PASSES_HALF + 2 * i), ("X", PASSES_HALF + 2 * i)] for i in range(PASSES_HALF // 2)]
+        whs = [("W", 2 * i) for i in range(PASSES_HALF // 2)]
+        non_h = []
+        if ORDER_KIND == 0:
             for q in range(QUARTERS):
-                for pp in range(2):
-                    non_h.append(("W", PASSES_HALF + q * PASSES_CHUNK + 2 * pp))
-                    non_h.append(("X", PASSES_HALF + q * PASSES_CHUNK + 2 * pp))
+                non_h += pairs[2 * q] + pairs[2 * q + 1]
                 if q < 2:
-                    for qq in (2 * q, 2 * q + 1):
-                        for pp in range(2):
-                            non_h.append(("W", qq * PASSES_CHUNK + 2 * pp))
-        elif NONH_ORDER == 1:
-            non_h = []
+                    non_h += whs[4 * q : 4 * q + 4]
+        elif ORDER_KIND == 1:
             for q in range(QUARTERS):
-                for pp in range(2):
-                    non_h.append(("W", PASSES_HALF + q * PASSES_CHUNK + 2 * pp))
-                    non_h.append(("X", PASSES_HALF + q * PASSES_CHUNK + 2 * pp))
-                for pp in range(2):
-                    non_h.append(("W", q * PASSES_CHUNK + 2 * pp))
+                non_h += pairs[2 * q] + pairs[2 * q + 1] + whs[2 * q : 2 * q + 2]
+        elif ORDER_KIND == 2:
+            for i in range(PASSES_HALF // 2):
+                non_h += pairs[i] + whs[i : i + 1]
+        elif ORDER_KIND == 3:
+            for q in range(QUARTERS):
+                non_h += whs[2 * q : 2 * q + 2] + pairs[2 * q] + pairs[2 * q + 1]
         else:
-            non_h = []
-            for q in range(QUARTERS):
-                for pp in range(2):
-                    non_h.append(("W", q * PASSES_CHUNK + 2 * pp))
-                for pp in range(2):
-                    non_h.append(("W", PASSES_HALF + q * PASSES_CHUNK + 2 * pp))
-                    non_h.append(("X", PASSES_HALF + q * PASSES_CHUNK + 2 * pp))
+            for i in range(PASSES_HALF // 2):
+                non_h += whs[i : i + 1] + pairs[i]
         h_steps = [(rt, part) for rt in range(ROW_TILES) for part in range(2)]
         order = []
         taken_h = 0
-        for s in range(n_steps):
-            if taken_h < len(h_steps) and (h_ready[h_steps[taken_h]] <= s or s - taken_h >= len(non_h)):
-                order.append(("H",) + h_steps[taken_h])
+        for s in range(len(non_h) + len(h_steps)):
+            if taken_h < len(h_steps) and (ripe[h_steps[taken_h]] <= s or s - taken_h >= len(non_h)):
+                rt, part = h_steps[taken_h]
+                order.append(("H", rt, part * BLOCKS_STEP, BLOCKS_STEP))
                 taken_h += 1
             else:
                 order.append(non_h[s - taken_h])
+        if SPLIT_LAST:
+            last = order[-1]
+            order[-1:] = [("H", last[1], last[2], BLOCKS_STEP // 2), ("H", last[1], last[2] + BLOCKS_STEP // 2, BLOCKS_STEP // 2)]
+        n_steps = len(order)
+        if WARM_EXP_AT < n_steps:
+            if LN_FIRST:
+                at(mid, WARM_EXP_AT, load_table, ACT.Ln)
+            at(mid, WARM_EXP_AT, load_table, ACT.Exp)
 
         raw = {}
+        uses = {}
+        source = {}
         fifo = []
         seen = set()
+
+        def want_mid(s):
+            for i, si in enumerate(piece_step):
+                if si == s:
+                    key = ("M", i // pieces, (i % pieces) * PIECE // CHUNK)
+                    if key not in seen:
+                        seen.add(key)
+                        fifo.append(key)
+
+        for s in range(MID_AHEAD):
+            want_mid(s)
+        narrow_left = 2 * NARROW
         for s, what in enumerate(order):
-            for i in relu_at.get(s + MID_AHEAD, []) + (relu_at.get(s, []) if s == 0 else []):
-                key = ("M", i // PIECES, (i % PIECES) * PIECE // CHUNK)
-                if key not in seen:
-                    seen.add(key)
-                    fifo.append(key)
+            want_mid(s + MID_AHEAD)
             if what[0] != "H":
-                key = (what[0], what[1] // PASSES_CHUNK)
+                if narrow_left > 0 or (what[1] % PASSES_CHUNK == 2 and (what[0], what[1] - 2, 2) in uses):
+                    narrow_left -= 1
+                    key = (what[0], what[1], 2)
+                else:
+                    key = (what[0], what[1] // PASSES_CHUNK * PASSES_CHUNK, PASSES_CHUNK)
+                source[s] = key
+                uses[key] = uses.get(key, 0) + 1
                 if key not in seen:
                     seen.add(key)
                     for rt in range(ROW_TILES):
                         fifo.append(key + (rt,))
-        for i in range(ROW_TILES * PIECES):
-            key = ("M", i // PIECES, (i % PIECES) * PIECE // CHUNK)
-            if key not in seen:
-                seen.add(key)
-                fifo.append(key)
         live = [0]
         loaded = [0]
 
@@ -178,60 +309,21 @@ def tile_bhcn_awx_pa_k_kernel(tc, mid_logits, x, W2, b2, out):
                     if live[0] >= RAW_BUFS:
                         return
                     live[0] += 1
-                    chunk = raw_pool.tile([P, CHUNK], BF16, tag="raw")
+                    width = key[2] * K_PASS
+                    chunk = raw_pool.tile([P, width], BF16, tag="raw")
                     src = W2 if key[0] == "W" else x
-                    col0 = key[1] * CHUNK if key[0] == "W" else (key[1] - QUARTERS) * CHUNK
-                    nc.sync.dma_start(out=chunk[:], in_=src[key[2] * P : (key[2] + 1) * P, col0 : col0 + CHUNK])
+                    col0 = key[1] * K_PASS if key[0] == "W" else (key[1] - PASSES_HALF) * K_PASS
+                    nc.sync.dma_start(out=chunk[:], in_=src[key[3] * P : (key[3] + 1) * P, col0 : col0 + width])
                     raw[key] = chunk
                 loaded[0] += 1
-
-        def relu_piece(i):
-            rt, j = i // PIECES, i % PIECES
-            cols = slice(j * PIECE, (j + 1) * PIECE)
-            nc.vector.tensor_scalar(
-                out=h[rt][:, cols], in0=h[rt][:, cols], scalar1=0.0, scalar2=None,
-                op0=ALU.max, op1=ALU.add, accum_out=sums[rt][:, j : j + 1],
-            )
-            if j == 0:
-                nc.vector.tensor_scalar_mul(out=neg_shift[rt][:], in0=sums[rt][:, 0:1], scalar1=-1.0 / PIECE)
-            if j == PIECES - 1:
-                nc.vector.tensor_reduce(out=total[rt][:], in_=sums[rt][:], axis=AX.X, op=ALU.add)
-                nc.vector.tensor_scalar_mul(out=neg_mean[rt][:], in0=total[rt][:], scalar1=-1.0 / L1)
-
-        def square_piece(i):
-            rt, j = i // PIECES, i % PIECES
-            cols = slice(j * PIECE, (j + 1) * PIECE)
-            scrap = scrap_pool.tile([P, PIECE], BF16, tag="scrap")
-            nc.scalar.activation(
-                out=scrap[:], in_=h[rt][:, cols], func=ACT.Square, bias=neg_shift[rt][:, 0:1], scale=1.0,
-                accum_out=squares[rt][:, j : j + 1],
-            )
-            if j == PIECES - 1:
-                nc.scalar.activation(out=gap2[rt][:], in_=total[rt][:], func=ACT.Square, bias=neg_shift[rt][:, 0:1], scale=1.0 / L1)
-
-        def stats_vector(rt):
-            nc.vector.tensor_reduce(out=spread[rt][:], in_=squares[rt][:], axis=AX.X, op=ALU.add)
-            nc.vector.scalar_tensor_tensor(
-                out=var[rt][:], in0=spread[rt][:], scalar=1.0 / L1, in1=gap2[rt][:], op0=ALU.mult, op1=ALU.subtract
-            )
-
-        def stats_scalar(rt):
-            nc.scalar.activation(out=std[rt][:], in_=var[rt][:], func=ACT.Sqrt, bias=LN_EPS, scale=1.0)
-
-        def scale_slice(rt, j):
-            if j == 0:
-                nc.vector.reciprocal(out=rstd[rt][:], in_=std[rt][:])
-            cols = slice(j * CHUNK, (j + 1) * CHUNK)
-            nc.vector.tensor_scalar(
-                out=h[rt][:, cols], in0=h[rt][:, cols], scalar1=neg_mean[rt][:, 0:1], scalar2=rstd[rt][:, 0:1],
-                op0=ALU.add, op1=ALU.mult,
-            )
 
         w_codes = {}
         r_codes = {}
         ready = []
+        done = [0]
         issued = [0] * ROW_TILES
         closed = []
+        fronted = [0]
 
         def multiply(rt, g):
             r_mx, r_col = r_codes[(rt, g)]
@@ -249,86 +341,65 @@ def tile_bhcn_awx_pa_k_kernel(tc, mid_logits, x, W2, b2, out):
             if issued[rt] == PASSES:
                 closed.append(rt)
 
-        done = [0]
-
-        def run_products(s):
-            while done[0] < len(ready) and ready[done[0]][0] <= s - LAG:
+        def run_products(latest, most):
+            n = 0
+            while done[0] < len(ready) and ready[done[0]][0] <= latest and n < most:
                 multiply(*ready[done[0]][1:])
                 done[0] += 1
-
-        bias = tail_pool.tile([P, L2], BF16)
-        exp_sums = tail_pool.tile([P, ROW_TILES], F32)
-        li = [tail_pool.tile([P, L2], F32, name="li%d" % rt) for rt in range(ROW_TILES)]
-        neg_max = [tail_pool.tile([P, 1], F32, name="neg_max%d" % rt) for rt in range(ROW_TILES)]
-
-        def softmax_front(rt):
-            nc.vector.tensor_tensor(out=li[rt][:], in0=acc[rt][:], in1=bias[:], op=ALU.add)
-            row_max = tail_pool.tile([P, 1], F32, name="row_max%d" % rt)
-            nc.vector.reduce_max(out=row_max[:], in_=li[rt][:], axis=AX.X)
-            nc.vector.tensor_scalar_mul(out=neg_max[rt][:], in0=row_max[:], scalar1=-1.0)
-            e = scrap_pool.tile([P, L2], F32, tag="scrap")
-            nc.scalar.activation(
-                out=e[:], in_=li[rt][:], func=ACT.Exp, bias=neg_max[rt][:, 0:1], scale=1.0,
-                accum_out=exp_sums[:, rt : rt + 1],
-            )
+                n += 1
 
         def block(rows, g):
             return rows[:].bitcast(F32)[:, g * WORDS_PASS : (g + 1) * WORDS_PASS]
 
         def step(s, what):
-            if what[0] == "W":
-                g0 = what[1]
-                q = g0 // PASSES_CHUNK
-                blocks = [block(raw[("W", q, rt)], (g0 + j) % PASSES_CHUNK) for j in range(2) for rt in range(ROW_TILES)]
-                pool = wx_pool if g0 >= PASSES_HALF else wh_pool
-            elif what[0] == "X":
-                g0 = what[1]
-                q = g0 // PASSES_CHUNK
-                blocks = [block(raw[("X", q, rt)], (g0 + j) % PASSES_CHUNK) for j in range(2) for rt in range(ROW_TILES)]
-                pool = xr_pool
-            else:
-                rt, part = what[1], what[2]
-                blocks = [block(h[rt], part * BLOCKS_STEP + j) for j in range(BLOCKS_STEP)]
+            if what[0] == "H":
+                rt0, g0, n_blocks = what[1], what[2], what[3]
+                blocks = [block(h[rt0], g0 + j) for j in range(n_blocks)]
                 pool = hr_pool
-            for i in relu_at.get(s, []):
-                relu_piece(i)
-            late = closed[:]
-            closed[:] = []
-            vector_banks = VB_DEFAULT
-            if VB2_EVERY and s % VB2_EVERY == VB2_EVERY - 1:
+            else:
+                g0 = what[1]
+                key = source[s]
+                n_blocks = BLOCKS_STEP
+                blocks = [block(raw[key + (rt,)], g0 + j - key[1]) for j in range(2) for rt in range(ROW_TILES)]
+                pool = xr_pool if what[0] == "X" else (wx_pool if g0 >= PASSES_HALF else wh_pool)
+            play(pre, s)
+            n_banks = n_blocks // 2
+            vector_banks = 1
+            if s in VB2_LIST:
                 vector_banks = 2
-            if s >= VB2_AFTER:
-                vector_banks = 2
-            grouped = group_pool.tile([P, BLOCKS_STEP * P * PACK], BF16, align_bytes=64, tag="grouped")
+            if s >= VB0_FROM:
+                vector_banks = 0
+            grouped = group_pool.tile([P, n_blocks * P * PACK], BF16, align_bytes=64, tag="grouped")
             grouped_words = grouped[:].bitcast(F32)
             bank_words = 2 * 2 * P
-            for t in range(BANKS_STEP):
+            for t in range(n_banks):
                 bank = bank_pool.tile([P, 2, 2, P], F32, tag="bank")
                 for a in range(2):
                     for u in range(2):
                         nc.tensor.transpose(bank[:, a, u, :], blocks[2 * t + a][:, u * P : (u + 1) * P], ident[:])
-                copy = nc.vector.tensor_copy if t >= BANKS_STEP - vector_banks else nc.scalar.copy
+                copy = nc.vector.tensor_copy if t >= n_banks - vector_banks else nc.scalar.copy
                 copy(
                     out=grouped_words[:, t * bank_words : (t + 1) * bank_words].rearrange(
                         "p (a r u) -> p a r u", a=2, u=2
                     ),
                     in_=bank[:].rearrange("p a u r -> p a r u"),
                 )
-            if s % RUN_EVERY == RUN_EVERY - 1:
-                run_products(s)
-            if s in stats_at:
-                stats_vector(stats_at[s])
-            for rt_j in scale_at.get(s, []):
-                scale_slice(*rt_j)
-            for rt in late:
-                softmax_front(rt)
-            for i in square_at.get(s, []):
-                square_piece(i)
-            if s in stats_at:
-                stats_scalar(stats_at[s])
-            codes = pool.tile([P, BLOCKS_STEP * P], U32, align_bytes=64, tag="codes")
-            scales = pool.tile([P, BLOCKS_STEP * P], U8, align_bytes=64, tag="scales")
+            if s < n_steps - TAIL_STEPS:
+                run_products(s - LAG, RUN_MAX)
+            else:
+                run_products(s - 1, 99)
+            play(gapb, s)
+            play(mid, s)
+            codes = pool.tile([P, n_blocks * P], U32, align_bytes=64, tag="codes")
+            scales = pool.tile([P, n_blocks * P], U8, align_bytes=64, tag="scales")
             nc.vector.quantize_mx(out=codes[:].bitcast(FP8X4), scales=scales[:], in_=grouped[:])
+            play(post, s)
+            if fronted[0] < len(closed):
+                front_add(closed[fronted[0]])
+                at(gapb, s + 1, front_max, closed[fronted[0]])
+                at(post, s + 1, front_neg, closed[fronted[0]])
+                at(mid, s + 2, front_scalar, closed[fronted[0]])
+                fronted[0] += 1
             mx = (codes, scales)
             if what[0] == "W":
                 for j in range(2):
@@ -345,13 +416,14 @@ def tile_bhcn_awx_pa_k_kernel(tc, mid_logits, x, W2, b2, out):
                         if g0 + j in w_codes:
                             ready.append((s, rt, g0 + j))
             else:
-                for j in range(BLOCKS_STEP):
-                    g = part * BLOCKS_STEP + j
-                    r_codes[(rt, g)] = (mx, j * P)
-                    if g in w_codes:
-                        ready.append((s, rt, g))
-            if what[0] != "H" and (what[1] % PASSES_CHUNK) == 2:
-                live[0] -= ROW_TILES
+                for j in range(n_blocks):
+                    r_codes[(rt0, g0 + j)] = (mx, j * P)
+                    if g0 + j in w_codes:
+                        ready.append((s, rt0, g0 + j))
+            if what[0] != "H":
+                uses[key] -= 1
+                if uses[key] == 0:
+                    live[0] -= ROW_TILES
 
         pump()
         for s, what in enumerate(order):
@@ -359,13 +431,20 @@ def tile_bhcn_awx_pa_k_kernel(tc, mid_logits, x, W2, b2, out):
                 nc.sync.dma_start(out=bias[:], in_=b2.partition_broadcast(P))
             step(s, what)
             pump()
-        run_products(n_steps + LAG)
-        for rt in closed:
-            softmax_front(rt)
+        run_products(n_steps, 999)
+        for s in (n_steps, n_steps + 1):
+            play(gapb, s)
+            play(mid, s)
+            play(post, s)
+        for rt in closed[fronted[0] :]:
+            front_add(rt)
+            front_max(rt)
+            front_neg(rt)
+            front_scalar(rt)
 
         log_sums = tail_pool.tile([P, ROW_TILES], F32)
         nc.scalar.activation(out=log_sums[:], in_=exp_sums[:], func=ACT.Ln)
-        for rt in range(ROW_TILES):
+        for rt in reversed(closed):
             nc.vector.tensor_scalar(
                 out=li[rt][:], in0=li[rt][:], scalar1=neg_max[rt][:, 0:1], scalar2=log_sums[:, rt : rt + 1],
                 op0=ALU.add, op1=ALU.subtract,

@@ -48,7 +48,7 @@ WX_BUFS = 3
 XR_BUFS = 3
 HR_BUFS = 3
 MID_AHEAD = 1
-NARROW = 2
+NARROW = 6
 SPLIT_LAST = 1
 ORDER_KIND = 0
 VB0_FROM = 99

@@ -39,7 +39,7 @@ SPREAD_TINY = 1
 SCALE_PER_STEP = 1
 FAST_FROM = 3
 RIPE_FAST = 2
-LAG = 1
+LAG = 2
 RUN_MAX = 5
 TAIL_STEPS = 4
 RAW_BUFS = 12
@@ -52,7 +52,7 @@ NARROW = 6
 SPLIT_LAST = 1
 ORDER_KIND = 0
 VB0_FROM = 99
-VB2_LIST = ()
+VB2_LIST = (2, 9, 16, 23)
 WARM_EXP_AT = 29
 LN_FIRST = 0
 SPLIT_FINAL = 0

@@ -30,6 +30,7 @@ BLOCKS_STEP = 8
 LN_EPS = 1e-5
 
 PIECE = 1024
+UNEVEN = 0
 NORM_NUM = 7
 NORM_DEN = 8
 R_OFF = 1
@@ -37,22 +38,33 @@ HEAD_DOUBLE = 0
 S_LAG = 1
 SPREAD_TINY = 1
 SCALE_PER_STEP = 1
+GP_SCALE = 0
+GP_PIECE = 1024
+VB2_EVERY = 0
+VB2_PHASE = 0
 FAST_FROM = 3
 RIPE_FAST = 2
 LAG = 2
 RUN_MAX = 5
+RUN_A = 0
+RUN_EVERY = 1
+DVE_BANK = 2
+VB_RULE = 2
 TAIL_STEPS = 4
 RAW_BUFS = 12
 GROUP_BUFS = 2
 WX_BUFS = 3
 XR_BUFS = 3
 HR_BUFS = 3
-MID_AHEAD = 1
+MID_AHEAD = 0
 NARROW = 6
-SPLIT_LAST = 1
+SPLIT_LAST = 0
 ORDER_KIND = 0
+NARROW_QUARTERS = 1
+ORDER_OVERRIDE = None
+PIECE_OVERRIDE = None
 VB0_FROM = 99
-VB2_LIST = (2, 9, 16, 23)
+VB2_LIST = ()
 WARM_EXP_AT = 29
 LN_FIRST = 0
 SPLIT_FINAL = 0
@@ -63,6 +75,11 @@ FLOPS = 2 * B * L2 * (L1 + D)
 def tile_bhcn_awx_pa_k_kernel(tc, mid_logits, x, W2, b2, out):
     nc = tc.nc
     pieces = L1 // PIECE
+    bounds = [j * PIECE for j in range(pieces + 1)]
+    if UNEVEN:
+        pieces = UNEVEN
+        width = L1 // pieces // P * P
+        bounds = [j * width for j in range(pieces)] + [L1]
     with ExitStack() as stack:
         const_pool = stack.enter_context(tc.tile_pool(name="const", bufs=1))
         raw_pool = stack.enter_context(tc.tile_pool(name="raw", bufs=RAW_BUFS))
@@ -104,14 +121,14 @@ def tile_bhcn_awx_pa_k_kernel(tc, mid_logits, x, W2, b2, out):
 
         def relu_piece(i):
             rt, j = i // pieces, i % pieces
-            cols = slice(j * PIECE, (j + 1) * PIECE)
+            cols = slice(bounds[j], bounds[j + 1])
             nc.vector.tensor_scalar(
                 out=h[rt][:, cols], in0=h[rt][:, cols], scalar1=0.0, scalar2=None,
                 op0=ALU.max, op1=ALU.add, accum_out=sums[rt][:, j : j + 1],
             )
 
         def shift(rt):
-            nc.vector.tensor_scalar_mul(out=neg_shift[rt][:], in0=sums[rt][:, 0:1], scalar1=-1.0 / PIECE)
+            nc.vector.tensor_scalar_mul(out=neg_shift[rt][:], in0=sums[rt][:, 0:1], scalar1=-1.0 / bounds[1])
 
         def row_total(rt):
             nc.vector.tensor_reduce(out=total[rt][:], in_=sums[rt][:], axis=AX.X, op=ALU.add)
@@ -121,8 +138,8 @@ def tile_bhcn_awx_pa_k_kernel(tc, mid_logits, x, W2, b2, out):
 
         def square_piece(i):
             rt, j = i // pieces, i % pieces
-            cols = slice(j * PIECE, (j + 1) * PIECE)
-            scrap = scrap_pool.tile([P, PIECE], BF16, tag="scrap")
+            cols = slice(bounds[j], bounds[j + 1])
+            scrap = scrap_pool.tile([P, bounds[j + 1] - bounds[j]], BF16, tag="scrap")
             nc.scalar.activation(
                 out=scrap[:], in_=h[rt][:, cols], func=ACT.Square, bias=neg_shift[rt][:, 0:1], scale=1.0,
                 accum_out=squares[rt][:, j : j + 1],
@@ -153,6 +170,13 @@ def tile_bhcn_awx_pa_k_kernel(tc, mid_logits, x, W2, b2, out):
             )
 
         row_max = [tail_pool.tile([P, 1], F32, name="row_max%d" % rt) for rt in range(ROW_TILES)]
+
+        def scale_on_gpsimd(rt):
+            for c0 in range(0, L1, GP_PIECE):
+                nc.gpsimd.tensor_scalar(
+                    out=h[rt][:, c0 : c0 + GP_PIECE], in0=h[rt][:, c0 : c0 + GP_PIECE],
+                    scalar1=neg_mean[rt][:, 0:1], scalar2=rstd[rt][:, 0:1], op0=ALU.add, op1=ALU.mult,
+                )
 
         def front_add(rt):
             nc.vector.tensor_tensor(out=li[rt][:], in0=acc[rt][:], in1=bias[:], op=ALU.add)
@@ -191,6 +215,8 @@ def tile_bhcn_awx_pa_k_kernel(tc, mid_logits, x, W2, b2, out):
                 piece_step.append(R_OFF + i // 2)
             else:
                 piece_step.append(R_OFF + HEAD_DOUBLE + ((i - 2 * HEAD_DOUBLE) * NORM_NUM) // NORM_DEN)
+        if PIECE_OVERRIDE:
+            piece_step = list(PIECE_OVERRIDE)
         ripe = {}
         n_pieces = ROW_TILES * pieces
         for i, s in enumerate(piece_step):
@@ -222,8 +248,11 @@ def tile_bhcn_awx_pa_k_kernel(tc, mid_logits, x, W2, b2, out):
                 at(gapb, a + S_LAG + 1, variance, rt)
                 at(mid, a + S_LAG + 1, deviation, rt)
                 at(post, a + S_LAG + 1, inverse, rt)
-                for j in range(QUARTERS):
-                    at(gapb, a + S_LAG + 2 + j // SCALE_PER_STEP, scale_slice, rt, j)
+                if GP_SCALE:
+                    at(post, a + S_LAG + 1, scale_on_gpsimd, rt)
+                else:
+                    for j in range(QUARTERS):
+                        at(gapb, a + S_LAG + 2 + j // SCALE_PER_STEP, scale_slice, rt, j)
                 ripe[(rt, 0)] = a + S_LAG + 3 + 1 // SCALE_PER_STEP
                 ripe[(rt, 1)] = a + S_LAG + 3 + 3 // SCALE_PER_STEP
         pairs = [[("W", PASSES_HALF + 2 * i), ("X", PASSES_HALF + 2 * i)] for i in range(PASSES_HALF // 2)]
@@ -243,9 +272,18 @@ def tile_bhcn_awx_pa_k_kernel(tc, mid_logits, x, W2, b2, out):
         elif ORDER_KIND == 3:
             for q in range(QUARTERS):
                 non_h += whs[2 * q : 2 * q + 2] + pairs[2 * q] + pairs[2 * q + 1]
-        else:
+        elif ORDER_KIND == 4:
             for i in range(PASSES_HALF // 2):
                 non_h += whs[i : i + 1] + pairs[i]
+        else:
+            for q in range(QUARTERS):
+                g = PASSES_HALF + q * PASSES_CHUNK
+                if q < NARROW_QUARTERS:
+                    non_h += pairs[2 * q] + pairs[2 * q + 1]
+                else:
+                    non_h += [("W", g), ("W", g + 2), ("Y", g, 0), ("Y", g, 1)]
+                if q < 2:
+                    non_h += whs[4 * q : 4 * q + 4]
         h_steps = [(rt, part) for rt in range(ROW_TILES) for part in range(2)]
         order = []
         taken_h = 0
@@ -256,6 +294,11 @@ def tile_bhcn_awx_pa_k_kernel(tc, mid_logits, x, W2, b2, out):
                 taken_h += 1
             else:
                 order.append(non_h[s - taken_h])
+        if ORDER_OVERRIDE:
+            order = list(ORDER_OVERRIDE)
+            for s, what in enumerate(order):
+                if what[0] == "H":
+                    assert ripe[(what[1], what[2] // BLOCKS_STEP)] <= s, "unripe"
         if SPLIT_LAST:
             last = order[-1]
             order[-1:] = [("H", last[1], last[2], BLOCKS_STEP // 2), ("H", last[1], last[2] + BLOCKS_STEP // 2, BLOCKS_STEP // 2)]
@@ -274,17 +317,26 @@ def tile_bhcn_awx_pa_k_kernel(tc, mid_logits, x, W2, b2, out):
         def want_mid(s):
             for i, si in enumerate(piece_step):
                 if si == s:
-                    key = ("M", i // pieces, (i % pieces) * PIECE // CHUNK)
-                    if key not in seen:
-                        seen.add(key)
-                        fifo.append(key)
+                    for q in range(bounds[i % pieces] // CHUNK, (bounds[i % pieces + 1] - 1) // CHUNK + 1):
+                        key = ("M", i // pieces, q)
+                        if key not in seen:
+                            seen.add(key)
+                            fifo.append(key)
 
         for s in range(MID_AHEAD):
             want_mid(s)
         narrow_left = 2 * NARROW
         for s, what in enumerate(order):
             want_mid(s + MID_AHEAD)
-            if what[0] != "H":
+            if what[0] == "Y":
+                key = ("X", what[1], PASSES_CHUNK)
+                source[s] = key
+                uses[key] = uses.get(key, 0) + 1
+                if key not in seen:
+                    seen.add(key)
+                    for rt in range(ROW_TILES):
+                        fifo.append(key + (rt,))
+            elif what[0] != "H":
                 if narrow_left > 0 or (what[1] % PASSES_CHUNK == 2 and (what[0], what[1] - 2, 2) in uses):
                     narrow_left -= 1
                     key = (what[0], what[1], 2)
@@ -356,6 +408,12 @@ def tile_bhcn_awx_pa_k_kernel(tc, mid_logits, x, W2, b2, out):
                 rt0, g0, n_blocks = what[1], what[2], what[3]
                 blocks = [block(h[rt0], g0 + j) for j in range(n_blocks)]
                 pool = hr_pool
+            elif what[0] == "Y":
+                g0 = what[1]
+                key = source[s]
+                n_blocks = BLOCKS_STEP
+                blocks = [block(raw[key + (2 * what[2] + a,)], j) for j in range(PASSES_CHUNK) for a in range(2)]
+                pool = xr_pool
             else:
                 g0 = what[1]
                 key = source[s]
@@ -365,7 +423,13 @@ def tile_bhcn_awx_pa_k_kernel(tc, mid_logits, x, W2, b2, out):
             play(pre, s)
             n_banks = n_blocks // 2
             vector_banks = 1
-            if s in VB2_LIST:
+            if s in VB2_LIST or (VB2_EVERY and s % VB2_EVERY == VB2_PHASE and s < n_steps - 4):
+                vector_banks = 2
+            if VB_RULE == 1 and s < n_steps - 4:
+                has_r = s in piece_step
+                has_s = (s - S_LAG) in piece_step
+                vector_banks = 2 if (has_s and not has_r) else (0 if (has_r and not has_s) else 1)
+            if VB_RULE == 2 and len([i for i in piece_step if i + S_LAG == s]) > 1:
                 vector_banks = 2
             if s >= VB0_FROM:
                 vector_banks = 0
@@ -377,15 +441,21 @@ def tile_bhcn_awx_pa_k_kernel(tc, mid_logits, x, W2, b2, out):
                 for a in range(2):
                     for u in range(2):
                         nc.tensor.transpose(bank[:, a, u, :], blocks[2 * t + a][:, u * P : (u + 1) * P], ident[:])
-                copy = nc.vector.tensor_copy if t >= n_banks - vector_banks else nc.scalar.copy
+                on_vector = t >= n_banks - vector_banks
+                if vector_banks == 1 and n_banks == 4:
+                    on_vector = t == DVE_BANK
+                copy = nc.vector.tensor_copy if on_vector else nc.scalar.copy
                 copy(
                     out=grouped_words[:, t * bank_words : (t + 1) * bank_words].rearrange(
                         "p (a r u) -> p a r u", a=2, u=2
                     ),
                     in_=bank[:].rearrange("p a u r -> p a r u"),
                 )
+                if RUN_A and t == 1 and s < n_steps - TAIL_STEPS:
+                    run_products(s - LAG, RUN_A)
             if s < n_steps - TAIL_STEPS:
-                run_products(s - LAG, RUN_MAX)
+                if s % RUN_EVERY == RUN_EVERY - 1:
+                    run_products(s - LAG, RUN_MAX)
             else:
                 run_products(s - 1, 99)
             play(gapb, s)
@@ -407,6 +477,12 @@ def tile_bhcn_awx_pa_k_kernel(tc, mid_logits, x, W2, b2, out):
                     for rt in range(ROW_TILES):
                         if (rt, g0 + j) in r_codes:
                             ready.append((s, rt, g0 + j))
+            elif what[0] == "Y":
+                for a in range(2):
+                    for j in range(PASSES_CHUNK):
+                        r_codes[(2 * what[2] + a, g0 + j)] = (mx, (2 * j + a) * P)
+                        if g0 + j in w_codes:
+                            ready.append((s, 2 * what[2] + a, g0 + j))
             elif what[0] == "X":
                 for j in range(2):
                     for rt in range(ROW_TILES):

@@ -35,6 +35,7 @@ NORM_NUM = 7
 NORM_DEN = 8
 R_OFF = 1
 HEAD_DOUBLE = 0
+HEAD_PAIRS = 3
 S_LAG = 1
 SPREAD_TINY = 1
 SCALE_PER_STEP = 1
@@ -209,12 +210,7 @@ def tile_bhcn_awx_pa_k_kernel(tc, mid_logits, x, W2, b2, out):
             for fn, args in where.get(s, []):
                 fn(*args)
 
-        piece_step = []
-        for i in range(ROW_TILES * pieces):
-            if i < 2 * HEAD_DOUBLE:
-                piece_step.append(R_OFF + i // 2)
-            else:
-                piece_step.append(R_OFF + HEAD_DOUBLE + ((i - 2 * HEAD_DOUBLE) * NORM_NUM) // NORM_DEN)
+        piece_step = [max(i // 2, i - HEAD_PAIRS) for i in range(ROW_TILES * pieces)]
         if PIECE_OVERRIDE:
             piece_step = list(PIECE_OVERRIDE)
         ripe = {}

@@ -36,6 +36,7 @@ NORM_DEN = 8
 R_OFF = 1
 HEAD_DOUBLE = 0
 HEAD_PAIRS = 3
+HOLD_BACK = 1
 S_LAG = 1
 SPREAD_TINY = 1
 SCALE_PER_STEP = 1
@@ -64,7 +65,7 @@ ORDER_KIND = 0
 NARROW_QUARTERS = 1
 ORDER_OVERRIDE = None
 PIECE_OVERRIDE = None
-VB0_FROM = 99
+VB0_FROM = 29
 VB2_LIST = ()
 WARM_EXP_AT = 29
 LN_FIRST = 0
@@ -251,6 +252,8 @@ def tile_bhcn_awx_pa_k_kernel(tc, mid_logits, x, W2, b2, out):
                         at(gapb, a + S_LAG + 2 + j // SCALE_PER_STEP, scale_slice, rt, j)
                 ripe[(rt, 0)] = a + S_LAG + 3 + 1 // SCALE_PER_STEP
                 ripe[(rt, 1)] = a + S_LAG + 3 + 3 // SCALE_PER_STEP
+        if HOLD_BACK:
+            ripe[(ROW_TILES - 2, 1)] = 29
         pairs = [[("W", PASSES_HALF + 2 * i), ("X", PASSES_HALF + 2 * i)] for i in range(PASSES_HALF // 2)]
         whs = [("W", 2 * i) for i in range(PASSES_HALF // 2)]
         non_h = []

from contextlib import ExitStack

import concourse.mybir as mybir
from concourse.masks import make_identity

F32 = mybir.dt.float32
BF16 = mybir.dt.bfloat16
U32 = mybir.dt.uint32
U8 = mybir.dt.uint8
FP8X4 = mybir.dt.float8_e4m3fn_x4
ACT = mybir.ActivationFunctionType
ALU = mybir.AluOpType
AX = mybir.AxisListType

P = 128
PACK = 4
K_PASS = P * PACK
WORDS_PASS = K_PASS // 2
B = 512
L1 = 8192
D = 8192
L2 = 512
ROW_TILES = B // P
CHUNK = 2048
QUARTERS = L1 // CHUNK
PASSES_CHUNK = CHUNK // K_PASS
PASSES_HALF = L1 // K_PASS
PASSES = 2 * PASSES_HALF
BLOCKS_STEP = 8
LN_EPS = 1e-5

PIECE = 1024
UNEVEN = 0
NORM_NUM = 7
NORM_DEN = 8
R_OFF = 1
HEAD_DOUBLE = 0
HEAD_PAIRS = 3
HOLD_BACK = 1
S_LAG = 1
SPREAD_TINY = 1
SCALE_PER_STEP = 1
GP_SCALE = 0
GP_PIECE = 1024
VB2_EVERY = 0
VB2_PHASE = 0
FAST_FROM = 3
RIPE_FAST = 2
LAG = 2
RUN_MAX = 5
RUN_A = 0
RUN_EVERY = 1
DVE_BANK = 2
VB_RULE = 2
TAIL_STEPS = 4
RAW_BUFS = 12
GROUP_BUFS = 2
WX_BUFS = 3
XR_BUFS = 3
HR_BUFS = 3
MID_AHEAD = 0
NARROW = 6
SPLIT_LAST = 0
ORDER_KIND = 0
NARROW_QUARTERS = 1
ORDER_OVERRIDE = None
PIECE_OVERRIDE = None
VB0_FROM = 29
VB2_LIST = ()
WARM_EXP_AT = 29
LN_FIRST = 0
SPLIT_FINAL = 0

FLOPS = 2 * B * L2 * (L1 + D)


def tile_bhcn_awx_pa_k_kernel(tc, mid_logits, x, W2, b2, out):
    nc = tc.nc
    pieces = L1 // PIECE
    bounds = [j * PIECE for j in range(pieces + 1)]
    if UNEVEN:
        pieces = UNEVEN
        width = L1 // pieces // P * P
        bounds = [j * width for j in range(pieces)] + [L1]
    with ExitStack() as stack:
        const_pool = stack.enter_context(tc.tile_pool(name="const", bufs=1))
        raw_pool = stack.enter_context(tc.tile_pool(name="raw", bufs=RAW_BUFS))
        norm_pool = stack.enter_context(tc.tile_pool(name="norm", bufs=1))
        scrap_pool = stack.enter_context(tc.tile_pool(name="scrap", bufs=2))
        group_pool = stack.enter_context(tc.tile_pool(name="group", bufs=GROUP_BUFS))
        wx_pool = stack.enter_context(tc.tile_pool(name="wx", bufs=WX_BUFS))
        wh_pool = stack.enter_context(tc.tile_pool(name="wh", bufs=PASSES_HALF // 2))
        xr_pool = stack.enter_context(tc.tile_pool(name="xr", bufs=XR_BUFS))
        hr_pool = stack.enter_context(tc.tile_pool(name="hr", bufs=HR_BUFS))
        tail_pool = stack.enter_context(tc.tile_pool(name="tail", bufs=1))
        acc_pool = stack.enter_context(tc.psum_pool(name="acc", bufs=1))
        bank_pool = stack.enter_context(tc.psum_pool(name="bank", bufs=4))
        stack.enter_context(tc.manual_schedule())

        ident = const_pool.tile([P, P], F32)
        make_identity(nc, ident[:])
        one = const_pool.tile([P, 1], F32)
        nc.vector.memset(one[:], 1.0)
        warm = const_pool.tile([P, 1], F32)
        nc.scalar.activation(out=warm[:], in_=one[:], func=ACT.Sqrt)

        acc = [acc_pool.tile([P, L2], F32, name="acc%d" % rt) for rt in range(ROW_TILES)]
        h = [norm_pool.tile([P, L1], BF16, name="h%d" % rt) for rt in range(ROW_TILES)]
        sums = [norm_pool.tile([P, pieces], F32, name="sums%d" % rt) for rt in range(ROW_TILES)]
        squares = [norm_pool.tile([P, pieces], F32, name="squares%d" % rt) for rt in range(ROW_TILES)]
        neg_shift = [norm_pool.tile([P, 1], F32, name="neg_shift%d" % rt) for rt in range(ROW_TILES)]
        neg_mean = [norm_pool.tile([P, 1], F32, name="neg_mean%d" % rt) for rt in range(ROW_TILES)]
        total = [norm_pool.tile([P, 1], F32, name="total%d" % rt) for rt in range(ROW_TILES)]
        gap2 = [norm_pool.tile([P, 1], F32, name="gap2%d" % rt) for rt in range(ROW_TILES)]
        spread = [norm_pool.tile([P, 1], F32, name="spread%d" % rt) for rt in range(ROW_TILES)]
        var = [norm_pool.tile([P, 1], F32, name="var%d" % rt) for rt in range(ROW_TILES)]
        std = [norm_pool.tile([P, 1], F32, name="std%d" % rt) for rt in range(ROW_TILES)]
        rstd = [norm_pool.tile([P, 1], F32, name="rstd%d" % rt) for rt in range(ROW_TILES)]
        bias = tail_pool.tile([P, L2], BF16)
        exp_sums = tail_pool.tile([P, ROW_TILES], F32)
        li = [tail_pool.tile([P, L2], F32, name="li%d" % rt) for rt in range(ROW_TILES)]
        neg_max = [tail_pool.tile([P, 1], F32, name="neg_max%d" % rt) for rt in range(ROW_TILES)]

        def relu_piece(i):
            rt, j = i // pieces, i % pieces
            cols = slice(bounds[j], bounds[j + 1])
            nc.vector.tensor_scalar(
                out=h[rt][:, cols], in0=h[rt][:, cols], scalar1=0.0, scalar2=None,
                op0=ALU.max, op1=ALU.add, accum_out=sums[rt][:, j : j + 1],
            )

        def shift(rt):
            nc.vector.tensor_scalar_mul(out=neg_shift[rt][:], in0=sums[rt][:, 0:1], scalar1=-1.0 / bounds[1])

        def row_total(rt):
            nc.vector.tensor_reduce(out=total[rt][:], in_=sums[rt][:], axis=AX.X, op=ALU.add)

        def mean(rt):
            nc.vector.tensor_scalar_mul(out=neg_mean[rt][:], in0=total[rt][:], scalar1=-1.0 / L1)

        def square_piece(i):
            rt, j = i // pieces, i % pieces
            cols = slice(bounds[j], bounds[j + 1])
            scrap = scrap_pool.tile([P, bounds[j + 1] - bounds[j]], BF16, tag="scrap")
            nc.scalar.activation(
                out=scrap[:], in_=h[rt][:, cols], func=ACT.Square, bias=neg_shift[rt][:, 0:1], scale=1.0,
                accum_out=squares[rt][:, j : j + 1],
            )

        def gap(rt):
            nc.scalar.activation(out=gap2[rt][:], in_=total[rt][:], func=ACT.Square, bias=neg_shift[rt][:, 0:1], scale=1.0 / L1)

        def row_spread(rt):
            nc.vector.tensor_reduce(out=spread[rt][:], in_=squares[rt][:], axis=AX.X, op=ALU.add)

        def variance(rt):
            nc.vector.scalar_tensor_tensor(
                out=var[rt][:], in0=spread[rt][:], scalar=1.0 / L1, in1=gap2[rt][:], op0=ALU.mult, op1=ALU.subtract
            )

        def deviation(rt):
            nc.scalar.activation(out=std[rt][:], in_=var[rt][:], func=ACT.Sqrt, bias=LN_EPS, scale=1.0)

        def inverse(rt):
            nc.vector.reciprocal(out=rstd[rt][:], in_=std[rt][:])

        def scale_slice(rt, j):
            cols = slice(j * CHUNK, (j + 1) * CHUNK)
            nc.vector.tensor_scalar(
                out=h[rt][:, cols], in0=h[rt][:, cols], scalar1=neg_mean[rt][:, 0:1], scalar2=rstd[rt][:, 0:1],
                op0=ALU.add, op1=ALU.mult,
            )

        row_max = [tail_pool.tile([P, 1], F32, name="row_max%d" % rt) for rt in range(ROW_TILES)]

        def scale_on_gpsimd(rt):
            for c0 in range(0, L1, GP_PIECE):
                nc.gpsimd.tensor_scalar(
                    out=h[rt][:, c0 : c0 + GP_PIECE], in0=h[rt][:, c0 : c0 + GP_PIECE],
                    scalar1=neg_mean[rt][:, 0:1], scalar2=rstd[rt][:, 0:1], op0=ALU.add, op1=ALU.mult,
                )

        def front_add(rt):
            nc.vector.tensor_tensor(out=li[rt][:], in0=acc[rt][:], in1=bias[:], op=ALU.add)

        def front_max(rt):
            nc.vector.reduce_max(out=row_max[rt][:], in_=li[rt][:], axis=AX.X)

        def front_neg(rt):
            nc.vector.tensor_scalar_mul(out=neg_max[rt][:], in0=row_max[rt][:], scalar1=-1.0)

        def front_scalar(rt):
            e = scrap_pool.tile([P, L2], F32, tag="scrap")
            nc.scalar.activation(
                out=e[:], in_=li[rt][:], func=ACT.Exp, bias=neg_max[rt][:, 0:1], scale=1.0,
                accum_out=exp_sums[:, rt : rt + 1],
            )

        def load_table(func):
            nc.scalar.activation(out=warm[:], in_=one[:], func=func)

        pre = {}
        gapb = {}
        mid = {}
        post = {}

        def at(where, s, fn, *args):
            where.setdefault(s, []).append((fn, args))

        def play(where, s):
            for fn, args in where.get(s, []):
                fn(*args)

        piece_step = [max(i // 2, i - HEAD_PAIRS) for i in range(ROW_TILES * pieces)]
        if PIECE_OVERRIDE:
            piece_step = list(PIECE_OVERRIDE)
        ripe = {}
        n_pieces = ROW_TILES * pieces
        for i, s in enumerate(piece_step):
            rt, j = i // pieces, i % pieces
            fast = rt >= FAST_FROM and j == pieces - 1
            at(gapb, s, relu_piece, i)
            at(mid, s if fast else s + S_LAG, square_piece, i)
            if j == 0:
                at(post, s, shift, rt)
        for rt in range(ROW_TILES):
            a = piece_step[rt * pieces + pieces - 1]
            if rt >= FAST_FROM:
                at(gapb, a, row_total, rt)
                at(mid, a, gap, rt)
                at(post, a, mean, rt)
                at(post, a, row_spread, rt)
                at(post, a, variance, rt)
                at(post, a, deviation, rt)
                at(pre, a + 1, inverse, rt)
                for j in range(QUARTERS):
                    at(pre, a + 1, scale_slice, rt, j)
                ripe[(rt, 0)] = a + RIPE_FAST
                ripe[(rt, 1)] = a + RIPE_FAST + 1
            else:
                at(post, a, row_total, rt)
                at(gapb, a + 1, mean, rt)
                at(mid, a + S_LAG, gap, rt)
                at(post, a + S_LAG, row_spread, rt)
                at(gapb, a + S_LAG + 1, variance, rt)
                at(mid, a + S_LAG + 1, deviation, rt)
                at(post, a + S_LAG + 1, inverse, rt)
                if GP_SCALE:
                    at(post, a + S_LAG + 1, scale_on_gpsimd, rt)
                else:
                    for j in range(QUARTERS):
                        at(gapb, a + S_LAG + 2 + j // SCALE_PER_STEP, scale_slice, rt, j)
                ripe[(rt, 0)] = a + S_LAG + 3 + 1 // SCALE_PER_STEP
                ripe[(rt, 1)] = a + S_LAG + 3 + 3 // SCALE_PER_STEP
        if HOLD_BACK:
            ripe[(ROW_TILES - 2, 1)] = 29
        pairs = [[("W", PASSES_HALF + 2 * i), ("X", PASSES_HALF + 2 * i)] for i in range(PASSES_HALF // 2)]
        whs = [("W", 2 * i) for i in range(PASSES_HALF // 2)]
        non_h = []
        if ORDER_KIND == 0:
            for q in range(QUARTERS):
                non_h += pairs[2 * q] + pairs[2 * q + 1]
                if q < 2:
                    non_h += whs[4 * q : 4 * q + 4]
        elif ORDER_KIND == 1:
            for q in range(QUARTERS):
                non_h += pairs[2 * q] + pairs[2 * q + 1] + whs[2 * q : 2 * q + 2]
        elif ORDER_KIND == 2:
            for i in range(PASSES_HALF // 2):
                non_h += pairs[i] + whs[i : i + 1]
        elif ORDER_KIND == 3:
            for q in range(QUARTERS):
                non_h += whs[2 * q : 2 * q + 2] + pairs[2 * q] + pairs[2 * q + 1]
        elif ORDER_KIND == 4:
            for i in range(PASSES_HALF // 2):
                non_h += whs[i : i + 1] + pairs[i]
        else:
            for q in range(QUARTERS):
                g = PASSES_HALF + q * PASSES_CHUNK
                if q < NARROW_QUARTERS:
                    non_h += pairs[2 * q] + pairs[2 * q + 1]
                else:
                    non_h += [("W", g), ("W", g + 2), ("Y", g, 0), ("Y", g, 1)]
                if q < 2:
                    non_h += whs[4 * q : 4 * q + 4]
        h_steps = [(rt, part) for rt in range(ROW_TILES) for part in range(2)]
        order = []
        taken_h = 0
        for s in range(len(non_h) + len(h_steps)):
            if taken_h < len(h_steps) and (ripe[h_steps[taken_h]] <= s or s - taken_h >= len(non_h)):
                rt, part = h_steps[taken_h]
                order.append(("H", rt, part * BLOCKS_STEP, BLOCKS_STEP))
                taken_h += 1
            else:
                order.append(non_h[s - taken_h])
        if ORDER_OVERRIDE:
            order = list(ORDER_OVERRIDE)
            for s, what in enumerate(order):
                if what[0] == "H":
                    assert ripe[(what[1], what[2] // BLOCKS_STEP)] <= s, "unripe"
        if SPLIT_LAST:
            last = order[-1]
            order[-1:] = [("H", last[1], last[2], BLOCKS_STEP // 2), ("H", last[1], last[2] + BLOCKS_STEP // 2, BLOCKS_STEP // 2)]
        n_steps = len(order)
        if WARM_EXP_AT < n_steps:
            if LN_FIRST:
                at(mid, WARM_EXP_AT, load_table, ACT.Ln)
            at(mid, WARM_EXP_AT, load_table, ACT.Exp)

        raw = {}
        uses = {}
        source = {}
        fifo = []
        seen = set()

        def want_mid(s):
            for i, si in enumerate(piece_step):
                if si == s:
                    for q in range(bounds[i % pieces] // CHUNK, (bounds[i % pieces + 1] - 1) // CHUNK + 1):
                        key = ("M", i // pieces, q)
                        if key not in seen:
                            seen.add(key)
                            fifo.append(key)

        for s in range(MID_AHEAD):
            want_mid(s)
        narrow_left = 2 * NARROW
        for s, what in enumerate(order):
            want_mid(s + MID_AHEAD)
            if what[0] == "Y":
                key = ("X", what[1], PASSES_CHUNK)
                source[s] = key
                uses[key] = uses.get(key, 0) + 1
                if key not in seen:
                    seen.add(key)
                    for rt in range(ROW_TILES):
                        fifo.append(key + (rt,))
            elif what[0] != "H":
                if narrow_left > 0 or (what[1] % PASSES_CHUNK == 2 and (what[0], what[1] - 2, 2) in uses):
                    narrow_left -= 1
                    key = (what[0], what[1], 2)
                else:
                    key = (what[0], what[1] // PASSES_CHUNK * PASSES_CHUNK, PASSES_CHUNK)
                source[s] = key
                uses[key] = uses.get(key, 0) + 1
                if key not in seen:
                    seen.add(key)
                    for rt in range(ROW_TILES):
                        fifo.append(key + (rt,))
        live = [0]
        loaded = [0]

        def pump():
            while loaded[0] < len(fifo):
                key = fifo[loaded[0]]
                if key[0] == "M":
                    cols = slice(key[2] * CHUNK, (key[2] + 1) * CHUNK)
                    nc.sync.dma_start(out=h[key[1]][:, cols], in_=mid_logits[key[1] * P : (key[1] + 1) * P, cols])
                else:
                    if live[0] >= RAW_BUFS:
                        return
                    live[0] += 1
                    width = key[2] * K_PASS
                    chunk = raw_pool.tile([P, width], BF16, tag="raw")
                    src = W2 if key[0] == "W" else x
                    col0 = key[1] * K_PASS if key[0] == "W" else (key[1] - PASSES_HALF) * K_PASS
                    nc.sync.dma_start(out=chunk[:], in_=src[key[3] * P : (key[3] + 1) * P, col0 : col0 + width])
                    raw[key] = chunk
                loaded[0] += 1

        w_codes = {}
        r_codes = {}
        ready = []
        done = [0]
        issued = [0] * ROW_TILES
        closed = []
        fronted = [0]

        def multiply(rt, g):
            r_mx, r_col = r_codes[(rt, g)]
            w_mx, w_col = w_codes[g]
            nc.tensor.matmul_mx(
                out=acc[rt][:],
                lhsT=r_mx[0][:, r_col : r_col + P].bitcast(FP8X4),
                lhsT_scale=r_mx[1][:, r_col : r_col + P],
                rhs=w_mx[0][:, w_col : w_col + L2].bitcast(FP8X4),
                rhs_scale=w_mx[1][:, w_col : w_col + L2],
                start=issued[rt] == 0,
                stop=issued[rt] == PASSES - 1,
            )
            issued[rt] += 1
            if issued[rt] == PASSES:
                closed.append(rt)

        def run_products(latest, most):
            n = 0
            while done[0] < len(ready) and ready[done[0]][0] <= latest and n < most:
                multiply(*ready[done[0]][1:])
                done[0] += 1
                n += 1

        def block(rows, g):
            return rows[:].bitcast(F32)[:, g * WORDS_PASS : (g + 1) * WORDS_PASS]

        def step(s, what):
            if what[0] == "H":
                rt0, g0, n_blocks = what[1], what[2], what[3]
                blocks = [block(h[rt0], g0 + j) for j in range(n_blocks)]
                pool = hr_pool
            elif what[0] == "Y":
                g0 = what[1]
                key = source[s]
                n_blocks = BLOCKS_STEP
                blocks = [block(raw[key + (2 * what[2] + a,)], j) for j in range(PASSES_CHUNK) for a in range(2)]
                pool = xr_pool
            else:
                g0 = what[1]
                key = source[s]
                n_blocks = BLOCKS_STEP
                blocks = [block(raw[key + (rt,)], g0 + j - key[1]) for j in range(2) for rt in range(ROW_TILES)]
                pool = xr_pool if what[0] == "X" else (wx_pool if g0 >= PASSES_HALF else wh_pool)
            play(pre, s)
            n_banks = n_blocks // 2
            vector_banks = 1
            if s in VB2_LIST or (VB2_EVERY and s % VB2_EVERY == VB2_PHASE and s < n_steps - 4):
                vector_banks = 2
            if VB_RULE == 1 and s < n_steps - 4:
                has_r = s in piece_step
                has_s = (s - S_LAG) in piece_step
                vector_banks = 2 if (has_s and not has_r) else (0 if (has_r and not has_s) else 1)
            if VB_RULE == 2 and len([i for i in piece_step if i + S_LAG == s]) > 1:
                vector_banks = 2
            if s >= VB0_FROM:
                vector_banks = 0
            grouped = group_pool.tile([P, n_blocks * P * PACK], BF16, align_bytes=64, tag="grouped")
            grouped_words = grouped[:].bitcast(F32)
            bank_words = 2 * 2 * P
            for t in range(n_banks):
                bank = bank_pool.tile([P, 2, 2, P], F32, tag="bank")
                for a in range(2):
                    for u in range(2):
                        nc.tensor.transpose(bank[:, a, u, :], blocks[2 * t + a][:, u * P : (u + 1) * P], ident[:])
                on_vector = t >= n_banks - vector_banks
                if vector_banks == 1 and n_banks == 4:
                    on_vector = t == DVE_BANK
                copy = nc.vector.tensor_copy if on_vector else nc.scalar.copy
                copy(
                    out=grouped_words[:, t * bank_words : (t + 1) * bank_words].rearrange(
                        "p (a r u) -> p a r u", a=2, u=2
                    ),
                    in_=bank[:].rearrange("p a u r -> p a r u"),
                )
                if RUN_A and t == 1 and s < n_steps - TAIL_STEPS:
                    run_products(s - LAG, RUN_A)
            if s < n_steps - TAIL_STEPS:
                if s % RUN_EVERY == RUN_EVERY - 1:
                    run_products(s - LAG, RUN_MAX)
            else:
                run_products(s - 1, 99)
            play(gapb, s)
            play(mid, s)
            codes = pool.tile([P, n_blocks * P], U32, align_bytes=64, tag="codes")
            scales = pool.tile([P, n_blocks * P], U8, align_bytes=64, tag="scales")
            nc.vector.quantize_mx(out=codes[:].bitcast(FP8X4), scales=scales[:], in_=grouped[:])
            play(post, s)
            if fronted[0] < len(closed):
                front_add(closed[fronted[0]])
                at(gapb, s + 1, front_max, closed[fronted[0]])
                at(post, s + 1, front_neg, closed[fronted[0]])
                at(mid, s + 2, front_scalar, closed[fronted[0]])
                fronted[0] += 1
            mx = (codes, scales)
            if what[0] == "W":
                for j in range(2):
                    w_codes[g0 + j] = (mx, j * L2)
                    for rt in range(ROW_TILES):
                        if (rt, g0 + j) in r_codes:
                            ready.append((s, rt, g0 + j))
            elif what[0] == "Y":
                for a in range(2):
                    for j in range(PASSES_CHUNK):
                        r_codes[(2 * what[2] + a, g0 + j)] = (mx, (2 * j + a) * P)
                        if g0 + j in w_codes:
                            ready.append((s, 2 * what[2] + a, g0 + j))
            elif what[0] == "X":
                for j in range(2):
                    for rt in range(ROW_TILES):
                        r_codes[(rt, g0 + j)] = (mx, (j * ROW_TILES + rt) * P)
                for rt in range(ROW_TILES):
                    for j in range(2):
                        if g0 + j in w_codes:
                            ready.append((s, rt, g0 + j))
            else:
                for j in range(n_blocks):
                    r_codes[(rt0, g0 + j)] = (mx, j * P)
                    if g0 + j in w_codes:
                        ready.append((s, rt0, g0 + j))
            if what[0] != "H":
                uses[key] -= 1
                if uses[key] == 0:
                    live[0] -= ROW_TILES

        pump()
        for s, what in enumerate(order):
            if s == 8:
                nc.sync.dma_start(out=bias[:], in_=b2.partition_broadcast(P))
            step(s, what)
            pump()
        run_products(n_steps, 999)
        for s in (n_steps, n_steps + 1):
            play(gapb, s)
            play(mid, s)
            play(post, s)
        for rt in closed[fronted[0] :]:
            front_add(rt)
            front_max(rt)
            front_neg(rt)
            front_scalar(rt)

        log_sums = tail_pool.tile([P, ROW_TILES], F32)
        nc.scalar.activation(out=log_sums[:], in_=exp_sums[:], func=ACT.Ln)
        for rt in reversed(closed):
            nc.vector.tensor_scalar(
                out=li[rt][:], in0=li[rt][:], scalar1=neg_max[rt][:, 0:1], scalar2=log_sums[:, rt : rt + 1],
                op0=ALU.add, op1=ALU.subtract,
            )
            nc.sync.dma_start(out=out[rt * P : (rt + 1) * P, :], in_=li[rt][:])
